import numpy as np
import ml_dtypes


def mxq(x, axis, fmt="e4m3"):
    dtype, down = {"e4m3": (ml_dtypes.float8_e4m3fn, 7), "e5m2": (ml_dtypes.float8_e5m2, 14)}[fmt]
    v = np.moveaxis(np.asarray(x, np.float32).astype(ml_dtypes.bfloat16).astype(np.float64), axis, -1)
    blocks = v.reshape(v.shape[:-1] + (-1, 32))
    amax = np.abs(blocks).max(-1, keepdims=True)
    byte = np.maximum(np.where(amax > 0, np.frexp(amax)[1] - 1 + 127, 0) - down, 1)
    scale = np.exp2(byte - 127.0)
    codes = (blocks / scale).astype(np.float32).astype(dtype).astype(np.float64)
    return np.moveaxis((codes * scale).reshape(v.shape), -1, axis)


WIDE = False


def mx_kscale(k):
    if not WIDE:
        return np.ones(k)
    levels = np.array([10, -10, 5, -5, 0])
    a = np.random.permutation(np.resize(levels, k // 512 * 4)).reshape(k // 512, 4)
    idx = np.arange(k)
    return np.exp2(a[idx // 512, idx % 128 // 32])


BF16 = ml_dtypes.bfloat16


def bf(x):
    return np.asarray(x, np.float32).astype(BF16)


def f64(x):
    return np.asarray(x).astype(np.float64)


B, N, DIM, H, DH, PD = 1, 512, 8192, 8, 64, 2
E = H * DH
ROT = DH // PD
INV_MIN_FREQ = 2.0 ** 6
EPS = 1e-5


def instance_norm(x):
    m = x.mean(axis=-1, keepdims=True)
    v = x.var(axis=-1, keepdims=True)
    return (x - m) * (1.0 / np.sqrt(v + EPS))


def rot_freqs(t):
    inv_freq = 1.0 / (10000.0 ** (np.arange(0, ROT, 2) / ROT))
    f = (t * INV_MIN_FREQ)[..., None] * inv_freq
    return np.concatenate([f, f], axis=-1)


def rotate_half(x):
    x1, x2 = np.split(x, 2, axis=-1)
    return np.concatenate([-x2, x1], axis=-1)


def apply_rotary(t, freqs):
    return t * np.cos(freqs) + rotate_half(t) * np.sin(freqs)


def rope_2d(t, pos):
    fx = rot_freqs(pos[..., 0])[:, None]
    fy = rot_freqs(pos[..., 1])[:, None]
    return np.concatenate([apply_rotary(t[..., :ROT], fx), apply_rotary(t[..., ROT:], fy)], axis=-1)


def heads(y):
    return y.reshape(B, N, H, DH).transpose(0, 2, 1, 3)


def setup_inputs():
    s = mx_kscale(DIM)
    return {"u_x": bf(np.random.standard_normal((B, N, DIM)) * s),
            "pos_x": bf(np.random.uniform(size=(1, N, PD))),
            "Wk": bf(np.random.standard_normal((E, DIM)) / np.sqrt(DIM) / s),
            "Wv": bf(np.random.standard_normal((E, DIM)) / np.sqrt(DIM) / s)}


def reference(u_x, pos_x, Wk, Wv):
    xq = mxq(f64(u_x), 2, "e4m3")
    k = heads(xq @ mxq(f64(Wk), 1, "e4m3").T)
    v = heads(xq @ mxq(f64(Wv), 1, "e4m3").T)
    k = instance_norm(k)
    v = instance_norm(v)
    k = rope_2d(k, f64(pos_x))
    return mxq(k, 2, "e4m3").transpose(0, 1, 3, 2) @ mxq(v, 2, "e4m3")

@@ -1,0 +1,295 @@
+import math
+from contextlib import ExitStack
+
+import concourse.mybir as mybir
+from concourse.masks import make_identity
+
+F32 = mybir.dt.float32
+BF16 = mybir.dt.bfloat16
+U32 = mybir.dt.uint32
+U8 = mybir.dt.uint8
+FP8X4 = mybir.dt.float8_e4m3fn_x4
+ALU = mybir.AluOpType
+ACT = mybir.ActivationFunctionType
+
+P = 128
+TOKENS = 512
+DIM = 8192
+CHANNELS = 512
+HEADS = 8
+HEAD = 64
+FREQS = 16
+ROW_TILES = 4
+K_PASS = 512
+PASSES = DIM // K_PASS
+WORDS = K_PASS // 2
+BANK = 512
+LOAD_PASSES = 2
+LOAD_K = LOAD_PASSES * K_PASS
+PAIRS = PASSES // LOAD_PASSES
+RAW_BUFS = 5
+EPS = 1e-5
+
+ROUND = 12582912.0
+TURN_HIGH = 6.28125
+TURN_LOW = 2.0 * math.pi - TURN_HIGH
+
+FLOPS = 2 * TOKENS * DIM * 2 * CHANNELS + 2 * HEADS * HEAD * HEAD * TOKENS
+
+
+def tile_asymetrickernel_pa_k_kernel(tc, u_x, pos_x, Wk, Wv, out):
+    nc = tc.nc
+    with ExitStack() as ctx:
+        ctx.enter_context(tc.manual_schedule())
+        keep = ctx.enter_context(tc.tile_pool(name="keep", bufs=1))
+        raw_pool = ctx.enter_context(tc.tile_pool(name="raw", bufs=RAW_BUFS))
+        grouped_pool = ctx.enter_context(tc.tile_pool(name="grouped", bufs=2))
+        small = ctx.enter_context(tc.tile_pool(name="small", bufs=ROW_TILES))
+        psum_k = ctx.enter_context(tc.psum_pool(name="psum_k", bufs=1))
+        psum_work = ctx.enter_context(tc.psum_pool(name="psum_work", bufs=4))
+
+        rows = {
+            "x": u_x[0].rearrange("(p t) k -> p t k", t=ROW_TILES),
+            "k": Wk.rearrange("(j p) k -> p j k", p=P),
+            "v": Wv.rearrange("(j p) k -> p j k", p=P),
+        }
+        codes = {}
+        scales = {}
+        for name in ("x", "k", "v"):
+            codes[name] = keep.tile([P, PASSES * BANK], U32, name="codes_" + name, align_bytes=64)
+            scales[name] = keep.tile([P, PASSES * BANK], U8, name="scales_" + name, align_bytes=64)
+
+        steps = [(name, pair) for pair in range(PAIRS) for name in ("x", "k", "v")]
+        raw_tiles = {}
+
+        def load(step):
+            name, pair = steps[step]
+            raw = raw_pool.tile([P, ROW_TILES * LOAD_K], BF16)
+            nc.sync.dma_start(
+                out=raw[:].rearrange("p (j k) -> p j k", j=ROW_TILES),
+                in_=rows[name][:, :, pair * LOAD_K : (pair + 1) * LOAD_K],
+            )
+            raw_tiles[step] = raw
+
+        for step in range(RAW_BUFS - 1):
+            load(step)
+
+        identity = keep.tile([P, P], F32)
+        make_identity(nc, identity[:])
+        eps = keep.tile([P, 1], F32)
+        nc.vector.memset(eps[:], EPS)
+
+        coords = ROW_TILES * 2
+        pos_bf = keep.tile([P, coords], BF16)
+        nc.scalar.dma_start(out=pos_bf[:], in_=pos_x[0].rearrange("(p t) d -> p (t d)", t=ROW_TILES))
+        pos = keep.tile([P, coords], F32)
+        nc.vector.tensor_copy(out=pos[:], in_=pos_bf[:])
+        angle = keep.tile([P, coords, FREQS], F32)
+        nc.vector.tensor_scalar(
+            out=angle[:, :, 0:1], in0=pos[:].unsqueeze(2), scalar1=64.0, scalar2=None, op0=ALU.mult
+        )
+        for w in (1, 2, 4, 8):
+            nc.vector.tensor_scalar(
+                out=angle[:, :, w : 2 * w],
+                in0=angle[:, :, 0:w],
+                scalar1=10000.0 ** (-w / FREQS),
+                scalar2=None,
+                op0=ALU.mult,
+            )
+        shifted = keep.tile([P, coords, FREQS], F32)
+        nc.vector.tensor_scalar(
+            out=shifted[:], in0=angle[:], scalar1=0.5 / math.pi, scalar2=ROUND, op0=ALU.mult, op1=ALU.add
+        )
+        turns = keep.tile([P, coords, FREQS], F32)
+        nc.vector.tensor_scalar(out=turns[:], in0=shifted[:], scalar1=ROUND, scalar2=None, op0=ALU.subtract)
+        rest_high = keep.tile([P, coords, FREQS], F32)
+        nc.vector.scalar_tensor_tensor(
+            out=rest_high[:], in0=turns[:], scalar=-TURN_HIGH, in1=angle[:], op0=ALU.mult, op1=ALU.add
+        )
+        rest = keep.tile([P, coords, FREQS], F32)
+        nc.vector.scalar_tensor_tensor(
+            out=rest[:], in0=turns[:], scalar=-TURN_LOW, in1=rest_high[:], op0=ALU.mult, op1=ALU.add
+        )
+        sin_half = keep.tile([P, coords, FREQS], F32)
+        nc.scalar.activation(out=sin_half[:], in_=rest[:], func=ACT.Sin, scale=0.5)
+        sin_quarter = keep.tile([P, coords, FREQS], F32)
+        nc.scalar.activation(out=sin_quarter[:], in_=rest[:], func=ACT.Sin, scale=0.25)
+        quarter_sq = keep.tile([P, coords, FREQS], F32)
+        nc.vector.tensor_tensor(out=quarter_sq[:], in0=sin_quarter[:], in1=sin_quarter[:], op=ALU.mult)
+        cos_half = keep.tile([P, coords, FREQS], F32)
+        nc.vector.tensor_scalar(
+            out=cos_half[:], in0=quarter_sq[:], scalar1=-2.0, scalar2=1.0, op0=ALU.mult, op1=ALU.add
+        )
+        half_sq = keep.tile([P, coords, FREQS], F32)
+        nc.vector.tensor_tensor(out=half_sq[:], in0=sin_half[:], in1=sin_half[:], op=ALU.mult)
+        half_product = keep.tile([P, coords, FREQS], F32)
+        nc.vector.tensor_tensor(out=half_product[:], in0=sin_half[:], in1=cos_half[:], op=ALU.mult)
+        cos_table = keep.tile([P, ROW_TILES, HEAD], F32)
+        sin_table = keep.tile([P, ROW_TILES, HEAD], F32)
+        cos_view = cos_table[:].rearrange("p t (d s j) -> p (t d) s j", d=2, s=2)
+        sin_view = sin_table[:].rearrange("p t (d s j) -> p (t d) s j", d=2, s=2)
+        for s in range(2):
+            nc.vector.tensor_scalar(
+                out=cos_view[:, :, s, :], in0=half_sq[:], scalar1=-2.0, scalar2=1.0, op0=ALU.mult, op1=ALU.add
+            )
+            nc.vector.tensor_scalar(
+                out=sin_view[:, :, s, :],
+                in0=half_product[:],
+                scalar1=(-2.0 if s == 0 else 2.0),
+                scalar2=None,
+                op0=ALU.mult,
+            )
+
+        def transpose_load(raw):
+            words = raw[:].bitcast(F32)
+            grouped = grouped_pool.tile([P, LOAD_PASSES * BANK * 4], BF16, align_bytes=64)
+            grouped_words = grouped[:].bitcast(F32)
+            for b in range(2 * LOAD_PASSES):
+                c_local, row_half = divmod(b, 2)
+                bank = psum_work.tile([P, BANK], F32)
+                for u in range(2):
+                    for jj in range(2):
+                        first = (2 * row_half + jj) * (LOAD_PASSES * WORDS) + c_local * WORDS + u * P
+                        nc.tensor.transpose(
+                            bank[:, (2 * u + jj) * P : (2 * u + jj + 1) * P], words[:, first : first + P], identity[:]
+                        )
+                copy = nc.vector.tensor_copy if b == 2 * LOAD_PASSES - 1 else nc.scalar.copy
+                copy(
+                    out=grouped_words[:, b * BANK : (b + 1) * BANK].rearrange("p (r u) -> p r u", u=2),
+                    in_=bank[:].rearrange("p (u r) -> p r u", u=2),
+                )
+            return grouped
+
+        def quantise(name, pair, grouped):
+            cols = slice(pair * LOAD_PASSES * BANK, (pair + 1) * LOAD_PASSES * BANK)
+            nc.vector.quantize_mx(out=codes[name][:, cols].bitcast(FP8X4), scales=scales[name][:, cols], in_=grouped[:])
+
+        def project(acc, weights, c, t):
+            tokens = slice(c * BANK + t * P, c * BANK + (t + 1) * P)
+            channels = slice(c * BANK, (c + 1) * BANK)
+            nc.tensor.matmul_mx(
+                out=acc[:],
+                lhsT=codes["x"][:, tokens].bitcast(FP8X4),
+                lhsT_scale=scales["x"][:, tokens],
+                rhs=codes[weights][:, channels].bitcast(FP8X4),
+                rhs_scale=scales[weights][:, channels],
+                start=(c == 0),
+                stop=(c == PASSES - 1),
+            )
+
+        k_acc = [psum_k.tile([P, BANK], F32, name="k_acc%d" % t) for t in range(ROW_TILES)]
+
+        def k_passes(c):
+            for t in range(ROW_TILES):
+                project(k_acc[t], "k", c, t)
+
+        waiting = None
+        for step, (name, pair) in enumerate(steps):
+            if step + RAW_BUFS - 1 < len(steps):
+                load(step + RAW_BUFS - 1)
+            if waiting is not None:
+                quantise(*waiting)
+            waiting = (name, pair, transpose_load(raw_tiles[step]))
+            if name == "v":
+                k_passes(LOAD_PASSES * pair)
+            if name == "x" and pair > 0:
+                k_passes(LOAD_PASSES * pair - 1)
+        quantise(*waiting)
+        k_passes(PASSES - 1)
+
+        def statistics(acc):
+            partial = small.tile([P, HEADS, 6], F32)
+            mean_var = small.tile([P, HEADS, 2], F32)
+            for h in range(HEADS):
+                nc.vector.bn_stats(out=partial[:, h, :], in_=acc[:, h * HEAD : (h + 1) * HEAD])
+            for h in range(HEADS):
+                nc.vector.bn_aggr(out=mean_var[:, h, :], in_=partial[:, h, :])
+            std = small.tile([P, HEADS], F32)
+            nc.scalar.activation(out=std[:], in_=mean_var[:, :, 1], func=ACT.Sqrt, bias=eps[:], scale=1.0)
+            return mean_var, std
+
+        def normalise(acc, mean_var, std, normed):
+            gain = small.tile([P, HEADS], F32)
+            nc.vector.reciprocal(out=gain[:], in_=std[:])
+            shift = small.tile([P, HEADS], F32)
+            nc.vector.scalar_tensor_tensor(
+                out=shift[:], in0=mean_var[:, :, 0], scalar=-1.0, in1=gain[:], op0=ALU.mult, op1=ALU.mult
+            )
+            for h in range(HEADS):
+                head = slice(h * HEAD, (h + 1) * HEAD)
+                nc.scalar.activation(
+                    out=normed[:, head], in_=acc[:, head], func=ACT.Identity, bias=shift[:, h : h + 1], scale=gain[:, h : h + 1]
+                )
+
+        k_normed = keep.tile([P, ROW_TILES, CHANNELS], F32)
+        k_stats = {}
+        for t in range(ROW_TILES + 1):
+            if t < ROW_TILES:
+                k_stats[t] = statistics(k_acc[t])
+            if t > 0:
+                normalise(k_acc[t - 1], k_stats[t - 1][0], k_stats[t - 1][1], k_normed[:, t - 1, :])
+
+        straight = keep.tile([P, ROW_TILES, CHANNELS], F32)
+        crossed = keep.tile([P, ROW_TILES, CHANNELS], F32)
+        for t in range(ROW_TILES):
+            nc.vector.tensor_tensor(
+                out=straight[:, t, :].rearrange("p (h c) -> p h c", h=HEADS),
+                in0=k_normed[:, t, :].rearrange("p (h c) -> p h c", h=HEADS),
+                in1=cos_table[:, t, :].unsqueeze(1).to_broadcast([P, HEADS, HEAD]),
+                op=ALU.mult,
+            )
+            y = k_normed[:, t, :].rearrange("p (h d s j) -> p h d s j", h=HEADS, d=2, s=2)
+            z = crossed[:, t, :].rearrange("p (h d s j) -> p h d s j", h=HEADS, d=2, s=2)
+            sines = sin_table[:, t, :].rearrange("p (d s j) -> p d s j", d=2, s=2)
+            for s in range(2):
+                nc.vector.tensor_tensor(
+                    out=z[:, :, :, s, :],
+                    in0=y[:, :, :, 1 - s, :],
+                    in1=sines[:, :, s, :].unsqueeze(1).to_broadcast([P, HEADS, 2, FREQS]),
+                    op=ALU.mult,
+                )
+        k_grouped = keep.tile([P, CHANNELS * ROW_TILES], BF16, align_bytes=64)
+        nc.vector.tensor_tensor(
+            out=k_grouped[:].rearrange("p (c t) -> p c t", t=ROW_TILES),
+            in0=straight[:].rearrange("p t c -> p c t"),
+            in1=crossed[:].rearrange("p t c -> p c t"),
+            op=ALU.add,
+        )
+        k_codes = keep.tile([P, CHANNELS], U32, align_bytes=64)
+        k_scales = keep.tile([P, CHANNELS], U8, align_bytes=64)
+        nc.vector.quantize_mx(out=k_codes[:].bitcast(FP8X4), scales=k_scales[:], in_=k_grouped[:])
+
+        v_normed = keep.tile([P, ROW_TILES, CHANNELS], BF16)
+        for t in range(ROW_TILES):
+            v_acc = psum_work.tile([P, BANK], F32, tag="bank")
+            for c in range(PASSES):
+                project(v_acc, "v", c, t)
+            mean_var, std = statistics(v_acc)
+            normalise(v_acc, mean_var, std, v_normed[:, t, :])
+        v_grouped = keep.tile([P, CHANNELS * ROW_TILES], BF16, align_bytes=64)
+        nc.vector.tensor_copy(
+            out=v_grouped[:].rearrange("p (c t) -> p c t", t=ROW_TILES), in_=v_normed[:].rearrange("p t c -> p c t")
+        )
+        v_codes = keep.tile([P, CHANNELS], U32, align_bytes=64)
+        v_scales = keep.tile([P, CHANNELS], U8, align_bytes=64)
+        nc.vector.quantize_mx(out=v_codes[:].bitcast(FP8X4), scales=v_scales[:], in_=v_grouped[:])
+
+        product = psum_work.tile([P, BANK], F32, tag="bank")
+        for g in range(HEADS // 2):
+            pair_cols = slice(g * P, (g + 1) * P)
+            nc.tensor.matmul_mx(
+                out=product[:, pair_cols],
+                lhsT=k_codes[:, pair_cols].bitcast(FP8X4),
+                lhsT_scale=k_scales[:, pair_cols],
+                rhs=v_codes[:, pair_cols].bitcast(FP8X4),
+                rhs_scale=v_scales[:, pair_cols],
+                start=True,
+                stop=True,
+            )
+        result = keep.tile([P, HEADS // 2, HEAD], F32)
+        blocks = product[:].rearrange("p (g n) -> p g n", n=P)
+        nc.vector.tensor_copy(out=result[0:HEAD, :, :], in_=blocks[0:HEAD, :, 0:HEAD])
+        nc.scalar.copy(out=result[HEAD:P, :, :], in_=blocks[HEAD:P, :, HEAD:P])
+        nc.sync.dma_start(
+            out=out.rearrange("b h c d -> (b h c) d").rearrange("(g p) d -> p g d", p=P), in_=result[:]
+        )

@@ -28,6 +28,7 @@ LOAD_PASSES = 2
 LOAD_K = LOAD_PASSES * K_PASS
 PAIRS = PASSES // LOAD_PASSES
 RAW_BUFS = 5
+MX_RUN = 3
 EPS = 1e-5
 
 ROUND = 12582912.0
@@ -179,11 +180,8 @@ def tile_asymetrickernel_pa_k_kernel(tc, u_x, pos_x, Wk, Wv, out):
 
         k_acc = [psum_k.tile([P, BANK], F32, name="k_acc%d" % t) for t in range(ROW_TILES)]
 
-        def k_passes(c):
-            for t in range(ROW_TILES):
-                project(k_acc[t], "k", c, t)
-
         waiting = None
+        ready = []
         for step, (name, pair) in enumerate(steps):
             if step + RAW_BUFS - 1 < len(steps):
                 load(step + RAW_BUFS - 1)
@@ -191,11 +189,13 @@ def tile_asymetrickernel_pa_k_kernel(tc, u_x, pos_x, Wk, Wv, out):
                 quantise(*waiting)
             waiting = (name, pair, transpose_load(raw_tiles[step]))
             if name == "v":
-                k_passes(LOAD_PASSES * pair)
-            if name == "x" and pair > 0:
-                k_passes(LOAD_PASSES * pair - 1)
+                ready.extend([(LOAD_PASSES * pair + i, t) for i in range(LOAD_PASSES) for t in range(ROW_TILES)])
+            for c, t in ready[:MX_RUN]:
+                project(k_acc[t], "k", c, t)
+            ready = ready[MX_RUN:]
         quantise(*waiting)
-        k_passes(PASSES - 1)
+        for c, t in ready:
+            project(k_acc[t], "k", c, t)
 
         def statistics(acc):
             partial = small.tile([P, HEADS, 6], F32)

@@ -24,11 +24,15 @@ K_PASS = 512
 PASSES = DIM // K_PASS
 WORDS = K_PASS // 2
 BANK = 512
+HALF = CHANNELS // 2
 LOAD_PASSES = 2
 LOAD_K = LOAD_PASSES * K_PASS
 PAIRS = PASSES // LOAD_PASSES
 RAW_BUFS = 5
-MX_RUN = 3
+SPLIT_LOADS = 2
+V_LAG = 2
+SINES_STEP = 1
+TABLES_STEP = 3
 EPS = 1e-5
 
 ROUND = 12582912.0
@@ -60,18 +64,29 @@ def tile_asymetrickernel_pa_k_kernel(tc, u_x, pos_x, Wk, Wv, out):
             codes[name] = keep.tile([P, PASSES * BANK], U32, name="codes_" + name, align_bytes=64)
             scales[name] = keep.tile([P, PASSES * BANK], U8, name="scales_" + name, align_bytes=64)
 
-        steps = [(name, pair) for pair in range(PAIRS) for name in ("x", "k", "v")]
+        steps = []
+        for i in range(PAIRS + V_LAG):
+            if i < PAIRS:
+                steps += [("x", i), ("k", i)]
+            if i >= V_LAG:
+                steps.append(("v", i - V_LAG))
         raw_tiles = {}
 
         def load(step):
             name, pair = steps[step]
-            raw = raw_pool.tile([P, ROW_TILES * LOAD_K], BF16)
-            nc.sync.dma_start(
-                out=raw[:].rearrange("p (j k) -> p j k", j=ROW_TILES),
-                in_=rows[name][:, :, pair * LOAD_K : (pair + 1) * LOAD_K],
-            )
-            raw_tiles[step] = raw
+            raw_tiles[step] = []
+            pieces = LOAD_PASSES if step < SPLIT_LOADS else 1
+            width = LOAD_K // pieces
+            for i in range(pieces):
+                bufs = RAW_BUFS if pieces == 1 else SPLIT_LOADS * LOAD_PASSES
+                raw = raw_pool.tile([P, ROW_TILES, width], BF16, name="raw%d" % pieces, bufs=bufs)
+                first = pair * LOAD_K + i * width
+                nc.sync.dma_start(out=raw[:], in_=rows[name][:, :, first : first + width])
+                raw_tiles[step].append(raw)
 
+        coords = ROW_TILES * 2
+        pos_bf = keep.tile([P, coords], BF16)
+        nc.scalar.dma_start(out=pos_bf[:], in_=pos_x[0].rearrange("(p t) d -> p (t d)", t=ROW_TILES))
         for step in range(RAW_BUFS - 1):
             load(step)
 
@@ -79,70 +94,78 @@ def tile_asymetrickernel_pa_k_kernel(tc, u_x, pos_x, Wk, Wv, out):
         make_identity(nc, identity[:])
         eps = keep.tile([P, 1], F32)
         nc.vector.memset(eps[:], EPS)
+        sin_table_load = keep.tile([P, 1], F32)
+        nc.scalar.activation(out=sin_table_load[:], in_=eps[:], func=ACT.Sin)
 
-        coords = ROW_TILES * 2
-        pos_bf = keep.tile([P, coords], BF16)
-        nc.scalar.dma_start(out=pos_bf[:], in_=pos_x[0].rearrange("(p t) d -> p (t d)", t=ROW_TILES))
-        pos = keep.tile([P, coords], F32)
-        nc.vector.tensor_copy(out=pos[:], in_=pos_bf[:])
-        angle = keep.tile([P, coords, FREQS], F32)
-        nc.vector.tensor_scalar(
-            out=angle[:, :, 0:1], in0=pos[:].unsqueeze(2), scalar1=64.0, scalar2=None, op0=ALU.mult
-        )
-        for w in (1, 2, 4, 8):
-            nc.vector.tensor_scalar(
-                out=angle[:, :, w : 2 * w],
-                in0=angle[:, :, 0:w],
-                scalar1=10000.0 ** (-w / FREQS),
-                scalar2=None,
-                op0=ALU.mult,
-            )
-        shifted = keep.tile([P, coords, FREQS], F32)
-        nc.vector.tensor_scalar(
-            out=shifted[:], in0=angle[:], scalar1=0.5 / math.pi, scalar2=ROUND, op0=ALU.mult, op1=ALU.add
-        )
-        turns = keep.tile([P, coords, FREQS], F32)
-        nc.vector.tensor_scalar(out=turns[:], in0=shifted[:], scalar1=ROUND, scalar2=None, op0=ALU.subtract)
-        rest_high = keep.tile([P, coords, FREQS], F32)
-        nc.vector.scalar_tensor_tensor(
-            out=rest_high[:], in0=turns[:], scalar=-TURN_HIGH, in1=angle[:], op0=ALU.mult, op1=ALU.add
-        )
-        rest = keep.tile([P, coords, FREQS], F32)
-        nc.vector.scalar_tensor_tensor(
-            out=rest[:], in0=turns[:], scalar=-TURN_LOW, in1=rest_high[:], op0=ALU.mult, op1=ALU.add
-        )
-        sin_half = keep.tile([P, coords, FREQS], F32)
-        nc.scalar.activation(out=sin_half[:], in_=rest[:], func=ACT.Sin, scale=0.5)
-        sin_quarter = keep.tile([P, coords, FREQS], F32)
-        nc.scalar.activation(out=sin_quarter[:], in_=rest[:], func=ACT.Sin, scale=0.25)
-        quarter_sq = keep.tile([P, coords, FREQS], F32)
-        nc.vector.tensor_tensor(out=quarter_sq[:], in0=sin_quarter[:], in1=sin_quarter[:], op=ALU.mult)
-        cos_half = keep.tile([P, coords, FREQS], F32)
-        nc.vector.tensor_scalar(
-            out=cos_half[:], in0=quarter_sq[:], scalar1=-2.0, scalar2=1.0, op0=ALU.mult, op1=ALU.add
-        )
-        half_sq = keep.tile([P, coords, FREQS], F32)
-        nc.vector.tensor_tensor(out=half_sq[:], in0=sin_half[:], in1=sin_half[:], op=ALU.mult)
-        half_product = keep.tile([P, coords, FREQS], F32)
-        nc.vector.tensor_tensor(out=half_product[:], in0=sin_half[:], in1=cos_half[:], op=ALU.mult)
         cos_table = keep.tile([P, ROW_TILES, HEAD], F32)
         sin_table = keep.tile([P, ROW_TILES, HEAD], F32)
-        cos_view = cos_table[:].rearrange("p t (d s j) -> p (t d) s j", d=2, s=2)
-        sin_view = sin_table[:].rearrange("p t (d s j) -> p (t d) s j", d=2, s=2)
-        for s in range(2):
-            nc.vector.tensor_scalar(
-                out=cos_view[:, :, s, :], in0=half_sq[:], scalar1=-2.0, scalar2=1.0, op0=ALU.mult, op1=ALU.add
-            )
-            nc.vector.tensor_scalar(
-                out=sin_view[:, :, s, :],
-                in0=half_product[:],
-                scalar1=(-2.0 if s == 0 else 2.0),
-                scalar2=None,
-                op0=ALU.mult,
-            )
 
-        def transpose_load(raw):
-            words = raw[:].bitcast(F32)
+        def reduced_angles():
+            pos = keep.tile([P, coords], F32)
+            nc.vector.tensor_copy(out=pos[:], in_=pos_bf[:])
+            angle = keep.tile([P, coords, FREQS], F32)
+            nc.vector.tensor_scalar(
+                out=angle[:, :, 0:1], in0=pos[:].unsqueeze(2), scalar1=64.0, scalar2=None, op0=ALU.mult
+            )
+            for w in (1, 2, 4, 8):
+                nc.vector.tensor_scalar(
+                    out=angle[:, :, w : 2 * w],
+                    in0=angle[:, :, 0:w],
+                    scalar1=10000.0 ** (-w / FREQS),
+                    scalar2=None,
+                    op0=ALU.mult,
+                )
+            shifted = keep.tile([P, coords, FREQS], F32)
+            nc.vector.tensor_scalar(
+                out=shifted[:], in0=angle[:], scalar1=0.5 / math.pi, scalar2=ROUND, op0=ALU.mult, op1=ALU.add
+            )
+            turns = keep.tile([P, coords, FREQS], F32)
+            nc.vector.tensor_scalar(out=turns[:], in0=shifted[:], scalar1=ROUND, scalar2=None, op0=ALU.subtract)
+            rest_high = keep.tile([P, coords, FREQS], F32)
+            nc.vector.scalar_tensor_tensor(
+                out=rest_high[:], in0=turns[:], scalar=-TURN_HIGH, in1=angle[:], op0=ALU.mult, op1=ALU.add
+            )
+            rest = keep.tile([P, coords, FREQS], F32)
+            nc.vector.scalar_tensor_tensor(
+                out=rest[:], in0=turns[:], scalar=-TURN_LOW, in1=rest_high[:], op0=ALU.mult, op1=ALU.add
+            )
+            return rest
+
+        def half_and_quarter_sines(rest):
+            sin_half = keep.tile([P, coords, FREQS], F32)
+            nc.scalar.activation(out=sin_half[:], in_=rest[:], func=ACT.Sin, scale=0.5)
+            sin_quarter = keep.tile([P, coords, FREQS], F32)
+            nc.scalar.activation(out=sin_quarter[:], in_=rest[:], func=ACT.Sin, scale=0.25)
+            return sin_half, sin_quarter
+
+        def rotary_tables(sin_half, sin_quarter):
+            quarter_sq = keep.tile([P, coords, FREQS], F32)
+            nc.vector.tensor_tensor(out=quarter_sq[:], in0=sin_quarter[:], in1=sin_quarter[:], op=ALU.mult)
+            cos_half = keep.tile([P, coords, FREQS], F32)
+            nc.vector.tensor_scalar(
+                out=cos_half[:], in0=quarter_sq[:], scalar1=-2.0, scalar2=1.0, op0=ALU.mult, op1=ALU.add
+            )
+            half_sq = keep.tile([P, coords, FREQS], F32)
+            nc.vector.tensor_tensor(out=half_sq[:], in0=sin_half[:], in1=sin_half[:], op=ALU.mult)
+            half_product = keep.tile([P, coords, FREQS], F32)
+            nc.vector.tensor_tensor(out=half_product[:], in0=sin_half[:], in1=cos_half[:], op=ALU.mult)
+            cos_view = cos_table[:].rearrange("p t (d s j) -> p (t d) s j", d=2, s=2)
+            sin_view = sin_table[:].rearrange("p t (d s j) -> p (t d) s j", d=2, s=2)
+            for s in range(2):
+                nc.vector.tensor_scalar(
+                    out=cos_view[:, :, s, :], in0=half_sq[:], scalar1=-2.0, scalar2=1.0, op0=ALU.mult, op1=ALU.add
+                )
+                nc.vector.tensor_scalar(
+                    out=sin_view[:, :, s, :],
+                    in0=half_product[:],
+                    scalar1=(-2.0 if s == 0 else 2.0),
+                    scalar2=None,
+                    op0=ALU.mult,
+                )
+
+        rest = reduced_angles()
+
+        def transpose_load(pieces):
             grouped = grouped_pool.tile([P, LOAD_PASSES * BANK * 4], BF16, align_bytes=64)
             grouped_words = grouped[:].bitcast(F32)
             for b in range(2 * LOAD_PASSES):
@@ -150,9 +173,14 @@ def tile_asymetrickernel_pa_k_kernel(tc, u_x, pos_x, Wk, Wv, out):
                 bank = psum_work.tile([P, BANK], F32)
                 for u in range(2):
                     for jj in range(2):
-                        first = (2 * row_half + jj) * (LOAD_PASSES * WORDS) + c_local * WORDS + u * P
+                        if len(pieces) == 1:
+                            words, first = pieces[0], c_local * WORDS + u * P
+                        else:
+                            words, first = pieces[c_local], u * P
                         nc.tensor.transpose(
-                            bank[:, (2 * u + jj) * P : (2 * u + jj + 1) * P], words[:, first : first + P], identity[:]
+                            bank[:, (2 * u + jj) * P : (2 * u + jj + 1) * P],
+                            words[:, 2 * row_half + jj, :].bitcast(F32)[:, first : first + P],
+                            identity[:],
                         )
                 copy = nc.vector.tensor_copy if b == 2 * LOAD_PASSES - 1 else nc.scalar.copy
                 copy(
@@ -165,9 +193,9 @@ def tile_asymetrickernel_pa_k_kernel(tc, u_x, pos_x, Wk, Wv, out):
             cols = slice(pair * LOAD_PASSES * BANK, (pair + 1) * LOAD_PASSES * BANK)
             nc.vector.quantize_mx(out=codes[name][:, cols].bitcast(FP8X4), scales=scales[name][:, cols], in_=grouped[:])
 
-        def project(acc, weights, c, t):
+        def project(acc, weights, c, t, first_channel, n_channels):
             tokens = slice(c * BANK + t * P, c * BANK + (t + 1) * P)
-            channels = slice(c * BANK, (c + 1) * BANK)
+            channels = slice(c * BANK + first_channel, c * BANK + first_channel + n_channels)
             nc.tensor.matmul_mx(
                 out=acc[:],
                 lhsT=codes["x"][:, tokens].bitcast(FP8X4),
@@ -178,7 +206,7 @@ def tile_asymetrickernel_pa_k_kernel(tc, u_x, pos_x, Wk, Wv, out):
                 stop=(c == PASSES - 1),
             )
 
-        k_acc = [psum_k.tile([P, BANK], F32, name="k_acc%d" % t) for t in range(ROW_TILES)]
+        k_acc = [psum_k.tile([P, BANK], F32, name="acc%d" % t) for t in range(ROW_TILES)]
 
         waiting = None
         ready = []
@@ -187,35 +215,44 @@ def tile_asymetrickernel_pa_k_kernel(tc, u_x, pos_x, Wk, Wv, out):
                 load(step + RAW_BUFS - 1)
             if waiting is not None:
                 quantise(*waiting)
+                if waiting[0] == "k":
+                    ready.extend(
+                        [(LOAD_PASSES * waiting[1] + i, t) for i in range(LOAD_PASSES) for t in range(ROW_TILES)]
+                    )
             waiting = (name, pair, transpose_load(raw_tiles[step]))
-            if name == "v":
-                ready.extend([(LOAD_PASSES * pair + i, t) for i in range(LOAD_PASSES) for t in range(ROW_TILES)])
-            for c, t in ready[:MX_RUN]:
-                project(k_acc[t], "k", c, t)
-            ready = ready[MX_RUN:]
-        quantise(*waiting)
-        for c, t in ready:
-            project(k_acc[t], "k", c, t)
+            run = 4 if step <= 2 * V_LAG else 3
+            if pair > PAIRS - 1 - V_LAG and name == "v":
+                run = len(ready)
+            for c, t in ready[:run]:
+                project(k_acc[t], "k", c, t, 0, CHANNELS)
+            ready = ready[run:]
+            if step == SINES_STEP:
+                half_and_quarter = half_and_quarter_sines(rest)
+                root_table = small.tile([P, 1], F32)
+                nc.scalar.activation(out=root_table[:], in_=eps[:], func=ACT.Abs_reciprocal_sqrt)
+            if step == TABLES_STEP:
+                rotary_tables(*half_and_quarter)
+        assert not ready
 
-        def statistics(acc):
-            partial = small.tile([P, HEADS, 6], F32)
-            mean_var = small.tile([P, HEADS, 2], F32)
-            for h in range(HEADS):
-                nc.vector.bn_stats(out=partial[:, h, :], in_=acc[:, h * HEAD : (h + 1) * HEAD])
-            for h in range(HEADS):
-                nc.vector.bn_aggr(out=mean_var[:, h, :], in_=partial[:, h, :])
-            std = small.tile([P, HEADS], F32)
-            nc.scalar.activation(out=std[:], in_=mean_var[:, :, 1], func=ACT.Sqrt, bias=eps[:], scale=1.0)
-            return mean_var, std
-
-        def normalise(acc, mean_var, std, normed):
-            gain = small.tile([P, HEADS], F32)
-            nc.vector.reciprocal(out=gain[:], in_=std[:])
-            shift = small.tile([P, HEADS], F32)
-            nc.vector.scalar_tensor_tensor(
-                out=shift[:], in0=mean_var[:, :, 0], scalar=-1.0, in1=gain[:], op0=ALU.mult, op1=ALU.mult
+        def statistics(acc, heads):
+            moments = small.tile([P, heads, 3], F32, name="moments%d" % heads)
+            for g in range(heads // 2):
+                nc.vector.bn_stats(
+                    out=moments[:, 2 * g : 2 * g + 2, :].rearrange("p h m -> p (h m)"),
+                    in_=acc[:, 2 * g * HEAD : (2 * g + 2) * HEAD].rearrange("p (h c) -> p c h", h=2),
+                )
+            gain = small.tile([P, heads], F32, name="gain%d" % heads)
+            nc.scalar.activation(
+                out=gain[:], in_=moments[:, :, 2], func=ACT.Abs_reciprocal_sqrt, bias=eps[:], scale=1.0 / HEAD
             )
-            for h in range(HEADS):
+            return moments[:, :, 1], gain
+
+        def normalise(acc, heads, mean, gain, normed):
+            shift = small.tile([P, heads], F32, name="shift%d" % heads)
+            nc.vector.scalar_tensor_tensor(
+                out=shift[:], in0=mean, scalar=-1.0, in1=gain[:], op0=ALU.mult, op1=ALU.mult
+            )
+            for h in range(heads):
                 head = slice(h * HEAD, (h + 1) * HEAD)
                 nc.scalar.activation(
                     out=normed[:, head], in_=acc[:, head], func=ACT.Identity, bias=shift[:, h : h + 1], scale=gain[:, h : h + 1]
@@ -225,9 +262,20 @@ def tile_asymetrickernel_pa_k_kernel(tc, u_x, pos_x, Wk, Wv, out):
         k_stats = {}
         for t in range(ROW_TILES + 1):
             if t < ROW_TILES:
-                k_stats[t] = statistics(k_acc[t])
+                k_stats[t] = statistics(k_acc[t], HEADS)
+            if t == 1:
+                quantise(*waiting)
             if t > 0:
-                normalise(k_acc[t - 1], k_stats[t - 1][0], k_stats[t - 1][1], k_normed[:, t - 1, :])
+                normalise(k_acc[t - 1], HEADS, k_stats[t - 1][0], k_stats[t - 1][1], k_normed[:, t - 1, :])
+
+        def multiply_v(half, t):
+            if half == 0:
+                v_acc = psum_work.tile([P, HALF], F32, tag="bank", name="v_acc")
+            else:
+                v_acc = psum_k.tile([P, HALF], F32, tag="acc%d" % t, name="v_acc")
+            for c in range(PASSES):
+                project(v_acc, "v", c, t, half * HALF, HALF)
+            return v_acc
 
         straight = keep.tile([P, ROW_TILES, CHANNELS], F32)
         crossed = keep.tile([P, ROW_TILES, CHANNELS], F32)
@@ -259,37 +307,46 @@ def tile_asymetrickernel_pa_k_kernel(tc, u_x, pos_x, Wk, Wv, out):
         k_scales = keep.tile([P, CHANNELS], U8, align_bytes=64)
         nc.vector.quantize_mx(out=k_codes[:].bitcast(FP8X4), scales=k_scales[:], in_=k_grouped[:])
 
-        v_normed = keep.tile([P, ROW_TILES, CHANNELS], BF16)
-        for t in range(ROW_TILES):
-            v_acc = psum_work.tile([P, BANK], F32, tag="bank")
-            for c in range(PASSES):
-                project(v_acc, "v", c, t)
-            mean_var, std = statistics(v_acc)
-            normalise(v_acc, mean_var, std, v_normed[:, t, :])
         v_grouped = keep.tile([P, CHANNELS * ROW_TILES], BF16, align_bytes=64)
-        nc.vector.tensor_copy(
-            out=v_grouped[:].rearrange("p (c t) -> p c t", t=ROW_TILES), in_=v_normed[:].rearrange("p t c -> p c t")
-        )
+        v_words = v_grouped[:].rearrange("p (c t) -> p c t", t=ROW_TILES)
         v_codes = keep.tile([P, CHANNELS], U32, align_bytes=64)
         v_scales = keep.tile([P, CHANNELS], U8, align_bytes=64)
-        nc.vector.quantize_mx(out=v_codes[:].bitcast(FP8X4), scales=v_scales[:], in_=v_grouped[:])
-
-        product = psum_work.tile([P, BANK], F32, tag="bank")
-        for g in range(HEADS // 2):
-            pair_cols = slice(g * P, (g + 1) * P)
-            nc.tensor.matmul_mx(
-                out=product[:, pair_cols],
-                lhsT=k_codes[:, pair_cols].bitcast(FP8X4),
-                lhsT_scale=k_scales[:, pair_cols],
-                rhs=v_codes[:, pair_cols].bitcast(FP8X4),
-                rhs_scale=v_scales[:, pair_cols],
-                start=True,
-                stop=True,
-            )
         result = keep.tile([P, HEADS // 2, HEAD], F32)
-        blocks = product[:].rearrange("p (g n) -> p g n", n=P)
-        nc.vector.tensor_copy(out=result[0:HEAD, :, :], in_=blocks[0:HEAD, :, 0:HEAD])
-        nc.scalar.copy(out=result[HEAD:P, :, :], in_=blocks[HEAD:P, :, HEAD:P])
-        nc.sync.dma_start(
-            out=out.rearrange("b h c d -> (b h c) d").rearrange("(g p) d -> p g d", p=P), in_=result[:]
-        )
+        out_rows = out.rearrange("b h c d -> (b h c) d").rearrange("(g p) d -> p g d", p=P)
+        half_heads = HEADS // 2
+
+        def finish(half):
+            cols = slice(half * HALF, (half + 1) * HALF)
+            words = slice(half * HALF * ROW_TILES, (half + 1) * HALF * ROW_TILES)
+            nc.vector.quantize_mx(out=v_codes[:, cols].bitcast(FP8X4), scales=v_scales[:, cols], in_=v_grouped[:, words])
+            product = psum_work.tile([P, HALF], F32, tag="bank", name="product")
+            for g in range(2):
+                pair_cols = slice(half * HALF + g * P, half * HALF + (g + 1) * P)
+                nc.tensor.matmul_mx(
+                    out=product[:, g * P : (g + 1) * P],
+                    lhsT=k_codes[:, pair_cols].bitcast(FP8X4),
+                    lhsT_scale=k_scales[:, pair_cols],
+                    rhs=v_codes[:, pair_cols].bitcast(FP8X4),
+                    rhs_scale=v_scales[:, pair_cols],
+                    start=True,
+                    stop=True,
+                )
+            blocks = product[:].rearrange("p (g n) -> p g n", n=P)
+            pairs = slice(2 * half, 2 * half + 2)
+            nc.vector.tensor_copy(out=result[0:HEAD, pairs, :], in_=blocks[0:HEAD, :, 0:HEAD])
+            nc.scalar.copy(out=result[HEAD:P, pairs, :], in_=blocks[HEAD:P, :, HEAD:P])
+            nc.sync.dma_start(out=out_rows[:, pairs, :], in_=result[:, pairs, :])
+
+        units = [(half, t) for half in range(2) for t in range(ROW_TILES)]
+        unnormed = None
+        for half, t in units + [(2, 0)]:
+            if half < 2:
+                v_acc = multiply_v(half, t)
+                mean, gain = statistics(v_acc, half_heads)
+            if unnormed is not None:
+                normalise(*unnormed)
+            if half < 2:
+                unnormed = (v_acc, half_heads, mean, gain, v_words[:, half * HALF : (half + 1) * HALF, t])
+            if (half, t) == (1, 2):
+                finish(0)
+        finish(1)

@@ -30,7 +30,8 @@ LOAD_K = LOAD_PASSES * K_PASS
 PAIRS = PASSES // LOAD_PASSES
 RAW_BUFS = 5
 SPLIT_LOADS = 2
-V_LAG = 2
+MX_RUNS = (4, 3)
+LATE_PASSES = 4
 SINES_STEP = 1
 TABLES_STEP = 3
 EPS = 1e-5
@@ -64,12 +65,9 @@ def tile_asymetrickernel_pa_k_kernel(tc, u_x, pos_x, Wk, Wv, out):
             codes[name] = keep.tile([P, PASSES * BANK], U32, name="codes_" + name, align_bytes=64)
             scales[name] = keep.tile([P, PASSES * BANK], U8, name="scales_" + name, align_bytes=64)
 
-        steps = []
-        for i in range(PAIRS + V_LAG):
-            if i < PAIRS:
-                steps += [("x", i), ("k", i)]
-            if i >= V_LAG:
-                steps.append(("v", i - V_LAG))
+        steps = [(name, pair) for pair in range(PAIRS) for name in ("x", "k")]
+        v_step = len(steps)
+        steps += [("v", pair) for pair in range(PAIRS)]
         raw_tiles = {}
 
         def load(step):
@@ -206,34 +204,6 @@ def tile_asymetrickernel_pa_k_kernel(tc, u_x, pos_x, Wk, Wv, out):
                 stop=(c == PASSES - 1),
             )
 
-        k_acc = [psum_k.tile([P, BANK], F32, name="acc%d" % t) for t in range(ROW_TILES)]
-
-        waiting = None
-        ready = []
-        for step, (name, pair) in enumerate(steps):
-            if step + RAW_BUFS - 1 < len(steps):
-                load(step + RAW_BUFS - 1)
-            if waiting is not None:
-                quantise(*waiting)
-                if waiting[0] == "k":
-                    ready.extend(
-                        [(LOAD_PASSES * waiting[1] + i, t) for i in range(LOAD_PASSES) for t in range(ROW_TILES)]
-                    )
-            waiting = (name, pair, transpose_load(raw_tiles[step]))
-            run = 4 if step <= 2 * V_LAG else 3
-            if pair > PAIRS - 1 - V_LAG and name == "v":
-                run = len(ready)
-            for c, t in ready[:run]:
-                project(k_acc[t], "k", c, t, 0, CHANNELS)
-            ready = ready[run:]
-            if step == SINES_STEP:
-                half_and_quarter = half_and_quarter_sines(rest)
-                root_table = small.tile([P, 1], F32)
-                nc.scalar.activation(out=root_table[:], in_=eps[:], func=ACT.Abs_reciprocal_sqrt)
-            if step == TABLES_STEP:
-                rotary_tables(*half_and_quarter)
-        assert not ready
-
         def statistics(acc, heads):
             moments = small.tile([P, heads, 3], F32, name="moments%d" % heads)
             for g in range(heads // 2):
@@ -258,24 +228,52 @@ def tile_asymetrickernel_pa_k_kernel(tc, u_x, pos_x, Wk, Wv, out):
                     out=normed[:, head], in_=acc[:, head], func=ACT.Identity, bias=shift[:, h : h + 1], scale=gain[:, h : h + 1]
                 )
 
+        k_acc = [psum_k.tile([P, BANK], F32, name="acc%d" % t) for t in range(ROW_TILES)]
+        accs = {("k", t): k_acc[t] for t in range(ROW_TILES)}
+
         k_normed = keep.tile([P, ROW_TILES, CHANNELS], F32)
         k_stats = {}
-        for t in range(ROW_TILES + 1):
-            if t < ROW_TILES:
-                k_stats[t] = statistics(k_acc[t], HEADS)
-            if t == 1:
-                quantise(*waiting)
-            if t > 0:
-                normalise(k_acc[t - 1], HEADS, k_stats[t - 1][0], k_stats[t - 1][1], k_normed[:, t - 1, :])
 
-        def multiply_v(half, t):
-            if half == 0:
-                v_acc = psum_work.tile([P, HALF], F32, tag="bank", name="v_acc")
-            else:
-                v_acc = psum_k.tile([P, HALF], F32, tag="acc%d" % t, name="v_acc")
-            for c in range(PASSES):
-                project(v_acc, "v", c, t, half * HALF, HALF)
-            return v_acc
+        waiting = None
+        ready = []
+        late = []
+        for step, (name, pair) in enumerate(steps):
+            if step + RAW_BUFS - 1 < len(steps):
+                load(step + RAW_BUFS - 1)
+            if waiting is not None:
+                quantise(*waiting)
+                passes = range(LOAD_PASSES * waiting[1], LOAD_PASSES * (waiting[1] + 1))
+                if waiting[0] == "k":
+                    for c in passes:
+                        for t in range(ROW_TILES):
+                            (ready if c < PASSES - LATE_PASSES else late).append(("k", c, t))
+                    if pair == 0 and name == "v":
+                        ready += sorted(late, key=lambda one: (one[2], one[1]))
+                if waiting[0] == "v":
+                    ready += [("v", c, t) for c in passes for t in range(2)]
+            if step == v_step + ROW_TILES:
+                for t in range(2):
+                    accs["v", t] = psum_k.tile([P, BANK], F32, tag="acc%d" % t, name="v_acc")
+            waiting = (name, pair, transpose_load(raw_tiles[step]))
+            run = MX_RUNS[step % 2] if step < v_step else 4
+            for weights, c, t in ready[:run]:
+                project(accs[weights, t], weights, c, t, 0, CHANNELS)
+            ready = ready[run:]
+            if step == SINES_STEP:
+                half_and_quarter = half_and_quarter_sines(rest)
+                root_table = small.tile([P, 1], F32)
+                nc.scalar.activation(out=root_table[:], in_=eps[:], func=ACT.Abs_reciprocal_sqrt)
+            if step == TABLES_STEP:
+                rotary_tables(*half_and_quarter)
+            t = step - v_step - 1
+            if 0 <= t < ROW_TILES:
+                k_stats[t] = statistics(k_acc[t], HEADS)
+            if 0 <= t - 1 < ROW_TILES:
+                normalise(k_acc[t - 1], HEADS, k_stats[t - 1][0], k_stats[t - 1][1], k_normed[:, t - 1, :])
+        quantise(*waiting)
+        ready += [("v", c, t) for c in range(PASSES - LOAD_PASSES, PASSES) for t in range(2)]
+        for weights, c, t in ready:
+            project(accs[weights, t], weights, c, t, 0, CHANNELS)
 
         straight = keep.tile([P, ROW_TILES, CHANNELS], F32)
         crossed = keep.tile([P, ROW_TILES, CHANNELS], F32)
@@ -313,7 +311,6 @@ def tile_asymetrickernel_pa_k_kernel(tc, u_x, pos_x, Wk, Wv, out):
         v_scales = keep.tile([P, CHANNELS], U8, align_bytes=64)
         result = keep.tile([P, HEADS // 2, HEAD], F32)
         out_rows = out.rearrange("b h c d -> (b h c) d").rearrange("(g p) d -> p g d", p=P)
-        half_heads = HEADS // 2
 
         def finish(half):
             cols = slice(half * HALF, (half + 1) * HALF)
@@ -337,16 +334,24 @@ def tile_asymetrickernel_pa_k_kernel(tc, u_x, pos_x, Wk, Wv, out):
             nc.scalar.copy(out=result[HEAD:P, pairs, :], in_=blocks[HEAD:P, :, HEAD:P])
             nc.sync.dma_start(out=out_rows[:, pairs, :], in_=result[:, pairs, :])
 
-        units = [(half, t) for half in range(2) for t in range(ROW_TILES)]
+        units = [(t, 0, CHANNELS) for t in range(2)]
+        units += [(t, half * HALF, HALF) for half in range(2) for t in range(2, ROW_TILES)]
         unnormed = None
-        for half, t in units + [(2, 0)]:
-            if half < 2:
-                v_acc = multiply_v(half, t)
-                mean, gain = statistics(v_acc, half_heads)
+        for t, first, width in units:
+            if t >= 2:
+                if first == 0:
+                    acc = psum_k.tile([P, HALF], F32, tag="acc%d" % t, name="v_acc")
+                else:
+                    acc = psum_work.tile([P, HALF], F32, tag="bank", name="v_acc")
+                for c in range(PASSES):
+                    project(acc, "v", c, t, first, width)
+            else:
+                acc = accs["v", t]
+            mean, gain = statistics(acc, width // HEAD)
             if unnormed is not None:
                 normalise(*unnormed)
-            if half < 2:
-                unnormed = (v_acc, half_heads, mean, gain, v_words[:, half * HALF : (half + 1) * HALF, t])
-            if (half, t) == (1, 2):
+            unnormed = (acc, width // HEAD, mean, gain, v_words[:, first : first + width, t])
+            if (t, first) == (2, HALF):
                 finish(0)
+        normalise(*unnormed)
         finish(1)

@@ -163,7 +163,7 @@ def tile_asymetrickernel_pa_k_kernel(tc, u_x, pos_x, Wk, Wv, out):
 
         rest = reduced_angles()
 
-        def transpose_load(pieces):
+        def transpose_load(pieces, vector_banks):
             grouped = grouped_pool.tile([P, LOAD_PASSES * BANK * 4], BF16, align_bytes=64)
             grouped_words = grouped[:].bitcast(F32)
             for b in range(2 * LOAD_PASSES):
@@ -180,7 +180,7 @@ def tile_asymetrickernel_pa_k_kernel(tc, u_x, pos_x, Wk, Wv, out):
                             words[:, 2 * row_half + jj, :].bitcast(F32)[:, first : first + P],
                             identity[:],
                         )
-                copy = nc.vector.tensor_copy if b == 2 * LOAD_PASSES - 1 else nc.scalar.copy
+                copy = nc.scalar.copy if b < 2 * LOAD_PASSES - vector_banks else nc.vector.tensor_copy
                 copy(
                     out=grouped_words[:, b * BANK : (b + 1) * BANK].rearrange("p (r u) -> p r u", u=2),
                     in_=bank[:].rearrange("p (u r) -> p r u", u=2),
@@ -228,10 +228,31 @@ def tile_asymetrickernel_pa_k_kernel(tc, u_x, pos_x, Wk, Wv, out):
                     out=normed[:, head], in_=acc[:, head], func=ACT.Identity, bias=shift[:, h : h + 1], scale=gain[:, h : h + 1]
                 )
 
+        k_normed = keep.tile([P, ROW_TILES, CHANNELS], F32)
+        straight = keep.tile([P, ROW_TILES, CHANNELS], F32)
+        crossed = keep.tile([P, ROW_TILES, CHANNELS], F32)
+
+        def rotate(t):
+            nc.vector.tensor_tensor(
+                out=straight[:, t, :].rearrange("p (h c) -> p h c", h=HEADS),
+                in0=k_normed[:, t, :].rearrange("p (h c) -> p h c", h=HEADS),
+                in1=cos_table[:, t, :].unsqueeze(1).to_broadcast([P, HEADS, HEAD]),
+                op=ALU.mult,
+            )
+            y = k_normed[:, t, :].rearrange("p (h d s j) -> p h d s j", h=HEADS, d=2, s=2)
+            z = crossed[:, t, :].rearrange("p (h d s j) -> p h d s j", h=HEADS, d=2, s=2)
+            sines = sin_table[:, t, :].rearrange("p (d s j) -> p d s j", d=2, s=2)
+            for s in range(2):
+                nc.vector.tensor_tensor(
+                    out=z[:, :, :, s, :],
+                    in0=y[:, :, :, 1 - s, :],
+                    in1=sines[:, :, s, :].unsqueeze(1).to_broadcast([P, HEADS, 2, FREQS]),
+                    op=ALU.mult,
+                )
+
         k_acc = [psum_k.tile([P, BANK], F32, name="acc%d" % t) for t in range(ROW_TILES)]
         accs = {("k", t): k_acc[t] for t in range(ROW_TILES)}
 
-        k_normed = keep.tile([P, ROW_TILES, CHANNELS], F32)
         k_stats = {}
 
         waiting = None
@@ -254,7 +275,8 @@ def tile_asymetrickernel_pa_k_kernel(tc, u_x, pos_x, Wk, Wv, out):
             if step == v_step + ROW_TILES:
                 for t in range(2):
                     accs["v", t] = psum_k.tile([P, BANK], F32, tag="acc%d" % t, name="v_acc")
-            waiting = (name, pair, transpose_load(raw_tiles[step]))
+            vector_banks = 1 if step < v_step + ROW_TILES else 0
+            waiting = (name, pair, transpose_load(raw_tiles[step], vector_banks))
             run = MX_RUNS[step % 2] if step < v_step else 4
             for weights, c, t in ready[:run]:
                 project(accs[weights, t], weights, c, t, 0, CHANNELS)
@@ -270,30 +292,13 @@ def tile_asymetrickernel_pa_k_kernel(tc, u_x, pos_x, Wk, Wv, out):
                 k_stats[t] = statistics(k_acc[t], HEADS)
             if 0 <= t - 1 < ROW_TILES:
                 normalise(k_acc[t - 1], HEADS, k_stats[t - 1][0], k_stats[t - 1][1], k_normed[:, t - 1, :])
+            if 0 <= t - 3 < ROW_TILES:
+                rotate(t - 3)
         quantise(*waiting)
         ready += [("v", c, t) for c in range(PASSES - LOAD_PASSES, PASSES) for t in range(2)]
         for weights, c, t in ready:
             project(accs[weights, t], weights, c, t, 0, CHANNELS)
 
-        straight = keep.tile([P, ROW_TILES, CHANNELS], F32)
-        crossed = keep.tile([P, ROW_TILES, CHANNELS], F32)
-        for t in range(ROW_TILES):
-            nc.vector.tensor_tensor(
-                out=straight[:, t, :].rearrange("p (h c) -> p h c", h=HEADS),
-                in0=k_normed[:, t, :].rearrange("p (h c) -> p h c", h=HEADS),
-                in1=cos_table[:, t, :].unsqueeze(1).to_broadcast([P, HEADS, HEAD]),
-                op=ALU.mult,
-            )
-            y = k_normed[:, t, :].rearrange("p (h d s j) -> p h d s j", h=HEADS, d=2, s=2)
-            z = crossed[:, t, :].rearrange("p (h d s j) -> p h d s j", h=HEADS, d=2, s=2)
-            sines = sin_table[:, t, :].rearrange("p (d s j) -> p d s j", d=2, s=2)
-            for s in range(2):
-                nc.vector.tensor_tensor(
-                    out=z[:, :, :, s, :],
-                    in0=y[:, :, :, 1 - s, :],
-                    in1=sines[:, :, s, :].unsqueeze(1).to_broadcast([P, HEADS, 2, FREQS]),
-                    op=ALU.mult,
-                )
         k_grouped = keep.tile([P, CHANNELS * ROW_TILES], BF16, align_bytes=64)
         nc.vector.tensor_tensor(
             out=k_grouped[:].rearrange("p (c t) -> p c t", t=ROW_TILES),
@@ -312,10 +317,12 @@ def tile_asymetrickernel_pa_k_kernel(tc, u_x, pos_x, Wk, Wv, out):
         result = keep.tile([P, HEADS // 2, HEAD], F32)
         out_rows = out.rearrange("b h c d -> (b h c) d").rearrange("(g p) d -> p g d", p=P)
 
-        def finish(half):
+        def quantise_v(half):
             cols = slice(half * HALF, (half + 1) * HALF)
             words = slice(half * HALF * ROW_TILES, (half + 1) * HALF * ROW_TILES)
             nc.vector.quantize_mx(out=v_codes[:, cols].bitcast(FP8X4), scales=v_scales[:, cols], in_=v_grouped[:, words])
+
+        def finish(half):
             product = psum_work.tile([P, HALF], F32, tag="bank", name="product")
             for g in range(2):
                 pair_cols = slice(half * HALF + g * P, half * HALF + (g + 1) * P)
@@ -352,6 +359,8 @@ def tile_asymetrickernel_pa_k_kernel(tc, u_x, pos_x, Wk, Wv, out):
                 normalise(*unnormed)
             unnormed = (acc, width // HEAD, mean, gain, v_words[:, first : first + width, t])
             if (t, first) == (2, HALF):
-                finish(0)
+                quantise_v(0)
         normalise(*unnormed)
+        finish(0)
+        quantise_v(1)
         finish(1)

@@ -32,7 +32,7 @@ RAW_BUFS = 5
 SPLIT_LOADS = 2
 MX_RUNS = (4, 3)
 LATE_PASSES = 4
-SINES_STEP = 1
+SINES_STEP = 3
 TABLES_STEP = 3
 EPS = 1e-5
 
@@ -100,13 +100,13 @@ def tile_asymetrickernel_pa_k_kernel(tc, u_x, pos_x, Wk, Wv, out):
 
         def reduced_angles():
             pos = keep.tile([P, coords], F32)
-            nc.vector.tensor_copy(out=pos[:], in_=pos_bf[:])
+            nc.gpsimd.tensor_copy(out=pos[:], in_=pos_bf[:])
             angle = keep.tile([P, coords, FREQS], F32)
-            nc.vector.tensor_scalar(
+            nc.gpsimd.tensor_scalar(
                 out=angle[:, :, 0:1], in0=pos[:].unsqueeze(2), scalar1=64.0, scalar2=None, op0=ALU.mult
             )
             for w in (1, 2, 4, 8):
-                nc.vector.tensor_scalar(
+                nc.gpsimd.tensor_scalar(
                     out=angle[:, :, w : 2 * w],
                     in0=angle[:, :, 0:w],
                     scalar1=10000.0 ** (-w / FREQS),
@@ -114,19 +114,18 @@ def tile_asymetrickernel_pa_k_kernel(tc, u_x, pos_x, Wk, Wv, out):
                     op0=ALU.mult,
                 )
             shifted = keep.tile([P, coords, FREQS], F32)
-            nc.vector.tensor_scalar(
+            nc.gpsimd.tensor_scalar(
                 out=shifted[:], in0=angle[:], scalar1=0.5 / math.pi, scalar2=ROUND, op0=ALU.mult, op1=ALU.add
             )
             turns = keep.tile([P, coords, FREQS], F32)
-            nc.vector.tensor_scalar(out=turns[:], in0=shifted[:], scalar1=ROUND, scalar2=None, op0=ALU.subtract)
-            rest_high = keep.tile([P, coords, FREQS], F32)
-            nc.vector.scalar_tensor_tensor(
-                out=rest_high[:], in0=turns[:], scalar=-TURN_HIGH, in1=angle[:], op0=ALU.mult, op1=ALU.add
-            )
-            rest = keep.tile([P, coords, FREQS], F32)
-            nc.vector.scalar_tensor_tensor(
-                out=rest[:], in0=turns[:], scalar=-TURN_LOW, in1=rest_high[:], op0=ALU.mult, op1=ALU.add
-            )
+            nc.gpsimd.tensor_scalar(out=turns[:], in0=shifted[:], scalar1=ROUND, scalar2=None, op0=ALU.subtract)
+            rest = angle
+            for i, part in enumerate((TURN_HIGH, TURN_LOW)):
+                turned = keep.tile([P, coords, FREQS], F32, name="turned%d" % i)
+                nc.gpsimd.tensor_scalar(out=turned[:], in0=turns[:], scalar1=part, scalar2=0.0, op0=ALU.mult, op1=ALU.add)
+                left = keep.tile([P, coords, FREQS], F32, name="left%d" % i)
+                nc.gpsimd.tensor_tensor(out=left[:], in0=rest[:], in1=turned[:], op=ALU.subtract)
+                rest = left
             return rest
 
         def half_and_quarter_sines(rest):
@@ -138,22 +137,22 @@ def tile_asymetrickernel_pa_k_kernel(tc, u_x, pos_x, Wk, Wv, out):
 
         def rotary_tables(sin_half, sin_quarter):
             quarter_sq = keep.tile([P, coords, FREQS], F32)
-            nc.vector.tensor_tensor(out=quarter_sq[:], in0=sin_quarter[:], in1=sin_quarter[:], op=ALU.mult)
+            nc.gpsimd.tensor_tensor(out=quarter_sq[:], in0=sin_quarter[:], in1=sin_quarter[:], op=ALU.mult)
             cos_half = keep.tile([P, coords, FREQS], F32)
-            nc.vector.tensor_scalar(
+            nc.gpsimd.tensor_scalar(
                 out=cos_half[:], in0=quarter_sq[:], scalar1=-2.0, scalar2=1.0, op0=ALU.mult, op1=ALU.add
             )
             half_sq = keep.tile([P, coords, FREQS], F32)
-            nc.vector.tensor_tensor(out=half_sq[:], in0=sin_half[:], in1=sin_half[:], op=ALU.mult)
+            nc.gpsimd.tensor_tensor(out=half_sq[:], in0=sin_half[:], in1=sin_half[:], op=ALU.mult)
             half_product = keep.tile([P, coords, FREQS], F32)
-            nc.vector.tensor_tensor(out=half_product[:], in0=sin_half[:], in1=cos_half[:], op=ALU.mult)
+            nc.gpsimd.tensor_tensor(out=half_product[:], in0=sin_half[:], in1=cos_half[:], op=ALU.mult)
             cos_view = cos_table[:].rearrange("p t (d s j) -> p (t d) s j", d=2, s=2)
             sin_view = sin_table[:].rearrange("p t (d s j) -> p (t d) s j", d=2, s=2)
             for s in range(2):
-                nc.vector.tensor_scalar(
+                nc.gpsimd.tensor_scalar(
                     out=cos_view[:, :, s, :], in0=half_sq[:], scalar1=-2.0, scalar2=1.0, op0=ALU.mult, op1=ALU.add
                 )
-                nc.vector.tensor_scalar(
+                nc.gpsimd.tensor_scalar(
                     out=sin_view[:, :, s, :],
                     in0=half_product[:],
                     scalar1=(-2.0 if s == 0 else 2.0),
@@ -217,6 +216,18 @@ def tile_asymetrickernel_pa_k_kernel(tc, u_x, pos_x, Wk, Wv, out):
             )
             return moments[:, :, 1], gain
 
+        def normalise_on_vector(acc, heads, mean, gain, normed):
+            for h in range(heads):
+                head = slice(h * HEAD, (h + 1) * HEAD)
+                nc.vector.tensor_scalar(
+                    out=normed[:, head],
+                    in0=acc[:, head],
+                    scalar1=mean[:, h : h + 1],
+                    scalar2=gain[:, h : h + 1],
+                    op0=ALU.subtract,
+                    op1=ALU.mult,
+                )
+
         def normalise(acc, heads, mean, gain, normed):
             shift = small.tile([P, heads], F32, name="shift%d" % heads)
             nc.vector.scalar_tensor_tensor(
@@ -229,16 +240,9 @@ def tile_asymetrickernel_pa_k_kernel(tc, u_x, pos_x, Wk, Wv, out):
                 )
 
         k_normed = keep.tile([P, ROW_TILES, CHANNELS], F32)
-        straight = keep.tile([P, ROW_TILES, CHANNELS], F32)
         crossed = keep.tile([P, ROW_TILES, CHANNELS], F32)
 
         def rotate(t):
-            nc.vector.tensor_tensor(
-                out=straight[:, t, :].rearrange("p (h c) -> p h c", h=HEADS),
-                in0=k_normed[:, t, :].rearrange("p (h c) -> p h c", h=HEADS),
-                in1=cos_table[:, t, :].unsqueeze(1).to_broadcast([P, HEADS, HEAD]),
-                op=ALU.mult,
-            )
             y = k_normed[:, t, :].rearrange("p (h d s j) -> p h d s j", h=HEADS, d=2, s=2)
             z = crossed[:, t, :].rearrange("p (h d s j) -> p h d s j", h=HEADS, d=2, s=2)
             sines = sin_table[:, t, :].rearrange("p (d s j) -> p d s j", d=2, s=2)
@@ -249,6 +253,13 @@ def tile_asymetrickernel_pa_k_kernel(tc, u_x, pos_x, Wk, Wv, out):
                     in1=sines[:, :, s, :].unsqueeze(1).to_broadcast([P, HEADS, 2, FREQS]),
                     op=ALU.mult,
                 )
+            straight = k_normed[:, t, :].rearrange("p (h c) -> p h c", h=HEADS)
+            nc.vector.tensor_tensor(
+                out=straight,
+                in0=straight,
+                in1=cos_table[:, t, :].unsqueeze(1).to_broadcast([P, HEADS, HEAD]),
+                op=ALU.mult,
+            )
 
         k_acc = [psum_k.tile([P, BANK], F32, name="acc%d" % t) for t in range(ROW_TILES)]
         accs = {("k", t): k_acc[t] for t in range(ROW_TILES)}
@@ -302,7 +313,7 @@ def tile_asymetrickernel_pa_k_kernel(tc, u_x, pos_x, Wk, Wv, out):
         k_grouped = keep.tile([P, CHANNELS * ROW_TILES], BF16, align_bytes=64)
         nc.vector.tensor_tensor(
             out=k_grouped[:].rearrange("p (c t) -> p c t", t=ROW_TILES),
-            in0=straight[:].rearrange("p t c -> p c t"),
+            in0=k_normed[:].rearrange("p t c -> p c t"),
             in1=crossed[:].rearrange("p t c -> p c t"),
             op=ALU.add,
         )
@@ -314,20 +325,20 @@ def tile_asymetrickernel_pa_k_kernel(tc, u_x, pos_x, Wk, Wv, out):
         v_words = v_grouped[:].rearrange("p (c t) -> p c t", t=ROW_TILES)
         v_codes = keep.tile([P, CHANNELS], U32, align_bytes=64)
         v_scales = keep.tile([P, CHANNELS], U8, align_bytes=64)
-        result = keep.tile([P, HEADS // 2, HEAD], F32)
-        out_rows = out.rearrange("b h c d -> (b h c) d").rearrange("(g p) d -> p g d", p=P)
+        result = keep.tile([P, 2, 2, P], F32)
+        out_heads = out[0].rearrange("(f g a) c d -> f a c g d", f=2, g=2)
 
         def quantise_v(half):
             cols = slice(half * HALF, (half + 1) * HALF)
             words = slice(half * HALF * ROW_TILES, (half + 1) * HALF * ROW_TILES)
             nc.vector.quantize_mx(out=v_codes[:, cols].bitcast(FP8X4), scales=v_scales[:, cols], in_=v_grouped[:, words])
 
-        def finish(half):
-            product = psum_work.tile([P, HALF], F32, tag="bank", name="product")
+        def finish(half, copies):
             for g in range(2):
                 pair_cols = slice(half * HALF + g * P, half * HALF + (g + 1) * P)
+                product = psum_work.tile([P, P], F32, tag="bank", name="product")
                 nc.tensor.matmul_mx(
-                    out=product[:, g * P : (g + 1) * P],
+                    out=product[:],
                     lhsT=k_codes[:, pair_cols].bitcast(FP8X4),
                     lhsT_scale=k_scales[:, pair_cols],
                     rhs=v_codes[:, pair_cols].bitcast(FP8X4),
@@ -335,11 +346,10 @@ def tile_asymetrickernel_pa_k_kernel(tc, u_x, pos_x, Wk, Wv, out):
                     start=True,
                     stop=True,
                 )
-            blocks = product[:].rearrange("p (g n) -> p g n", n=P)
-            pairs = slice(2 * half, 2 * half + 2)
-            nc.vector.tensor_copy(out=result[0:HEAD, pairs, :], in_=blocks[0:HEAD, :, 0:HEAD])
-            nc.scalar.copy(out=result[HEAD:P, pairs, :], in_=blocks[HEAD:P, :, HEAD:P])
-            nc.sync.dma_start(out=out_rows[:, pairs, :], in_=result[:, pairs, :])
+                copies[g](out=result[:, half, g, :], in_=product[:])
+            for a, dma in enumerate((nc.sync.dma_start, nc.scalar.dma_start)):
+                block = slice(a * HEAD, (a + 1) * HEAD)
+                dma(out=out_heads[half, a], in_=result[block, half, :, block])
 
         units = [(t, 0, CHANNELS) for t in range(2)]
         units += [(t, half * HALF, HALF) for half in range(2) for t in range(2, ROW_TILES)]
@@ -356,11 +366,12 @@ def tile_asymetrickernel_pa_k_kernel(tc, u_x, pos_x, Wk, Wv, out):
                 acc = accs["v", t]
             mean, gain = statistics(acc, width // HEAD)
             if unnormed is not None:
-                normalise(*unnormed)
+                norm(*unnormed)
+            norm = normalise if t < 2 else normalise_on_vector
             unnormed = (acc, width // HEAD, mean, gain, v_words[:, first : first + width, t])
             if (t, first) == (2, HALF):
                 quantise_v(0)
-        normalise(*unnormed)
-        finish(0)
+        finish(0, (nc.scalar.copy, nc.scalar.copy))
+        norm(*unnormed)
         quantise_v(1)
-        finish(1)
+        finish(1, (nc.vector.tensor_copy, nc.scalar.copy))

@@ -162,7 +162,7 @@ def tile_asymetrickernel_pa_k_kernel(tc, u_x, pos_x, Wk, Wv, out):
 
         rest = reduced_angles()
 
-        def transpose_load(pieces, vector_banks):
+        def transpose_load(pieces, vector_banks, run):
             grouped = grouped_pool.tile([P, LOAD_PASSES * BANK * 4], BF16, align_bytes=64)
             grouped_words = grouped[:].bitcast(F32)
             for b in range(2 * LOAD_PASSES):
@@ -184,6 +184,11 @@ def tile_asymetrickernel_pa_k_kernel(tc, u_x, pos_x, Wk, Wv, out):
                     out=grouped_words[:, b * BANK : (b + 1) * BANK].rearrange("p (r u) -> p r u", u=2),
                     in_=bank[:].rearrange("p (u r) -> p r u", u=2),
                 )
+                if b == LOAD_PASSES - 1:
+                    multiply_ready((run + 1) // 2)
+                    ready.extend(fresh)
+                    fresh.clear()
+            multiply_ready(run // 2)
             return grouped
 
         def quantise(name, pair, grouped):
@@ -268,7 +273,15 @@ def tile_asymetrickernel_pa_k_kernel(tc, u_x, pos_x, Wk, Wv, out):
 
         waiting = None
         ready = []
+        fresh = []
         late = []
+
+        def multiply_ready(count):
+            for weights, c, t in ready[:count]:
+                project(accs[weights, t], weights, c, t, 0, CHANNELS)
+            for one in ready[:count]:
+                ready.remove(one)
+
         for step, (name, pair) in enumerate(steps):
             if step + RAW_BUFS - 1 < len(steps):
                 load(step + RAW_BUFS - 1)
@@ -278,20 +291,17 @@ def tile_asymetrickernel_pa_k_kernel(tc, u_x, pos_x, Wk, Wv, out):
                 if waiting[0] == "k":
                     for c in passes:
                         for t in range(ROW_TILES):
-                            (ready if c < PASSES - LATE_PASSES else late).append(("k", c, t))
+                            (fresh if c < PASSES - LATE_PASSES else late).append(("k", c, t))
                     if pair == 0 and name == "v":
-                        ready += sorted(late, key=lambda one: (one[2], one[1]))
+                        fresh += sorted(late, key=lambda one: (one[2], one[1]))
                 if waiting[0] == "v":
-                    ready += [("v", c, t) for c in passes for t in range(2)]
+                    fresh += [("v", c, t) for c in passes for t in range(2)]
             if step == v_step + ROW_TILES:
                 for t in range(2):
                     accs["v", t] = psum_k.tile([P, BANK], F32, tag="acc%d" % t, name="v_acc")
             vector_banks = 1 if step < v_step + ROW_TILES else 0
-            waiting = (name, pair, transpose_load(raw_tiles[step], vector_banks))
             run = MX_RUNS[step % 2] if step < v_step else 4
-            for weights, c, t in ready[:run]:
-                project(accs[weights, t], weights, c, t, 0, CHANNELS)
-            ready = ready[run:]
+            waiting = (name, pair, transpose_load(raw_tiles[step], vector_banks, run))
             if step == SINES_STEP:
                 half_and_quarter = half_and_quarter_sines(rest)
                 root_table = small.tile([P, 1], F32)

@@ -32,8 +32,7 @@ RAW_BUFS = 5
 SPLIT_LOADS = 2
 MX_RUNS = (4, 3)
 LATE_PASSES = 4
-SINES_STEP = 3
-TABLES_STEP = 3
+ROTARY_STEP = 4
 EPS = 1e-5
 
 ROUND = 12582912.0
@@ -97,62 +96,68 @@ def tile_asymetrickernel_pa_k_kernel(tc, u_x, pos_x, Wk, Wv, out):
 
         cos_table = keep.tile([P, ROW_TILES, HEAD], F32)
         sin_table = keep.tile([P, ROW_TILES, HEAD], F32)
+        angle = keep.tile([P, coords, FREQS], F32)
+        shifted = keep.tile([P, coords, FREQS], F32)
+        turns = keep.tile([P, coords, FREQS], F32)
+        turned = [keep.tile([P, coords, FREQS], F32, name="turned%d" % i) for i in range(2)]
+        rest = [keep.tile([P, coords, FREQS], F32, name="rest%d" % i) for i in range(2)]
+        sin_half = keep.tile([P, coords, FREQS], F32)
+        sin_quarter = keep.tile([P, coords, FREQS], F32)
+        quarter_sq = keep.tile([P, coords, FREQS], F32)
+        cos_half = keep.tile([P, coords, FREQS], F32)
+        half_sq = keep.tile([P, coords, FREQS], F32)
+        half_product = keep.tile([P, coords, FREQS], F32)
 
-        def reduced_angles():
+        def angles():
             pos = keep.tile([P, coords], F32)
-            nc.gpsimd.tensor_copy(out=pos[:], in_=pos_bf[:])
-            angle = keep.tile([P, coords, FREQS], F32)
-            nc.gpsimd.tensor_scalar(
+            nc.vector.tensor_copy(out=pos[:], in_=pos_bf[:])
+            nc.vector.tensor_scalar(
                 out=angle[:, :, 0:1], in0=pos[:].unsqueeze(2), scalar1=64.0, scalar2=None, op0=ALU.mult
             )
             for w in (1, 2, 4, 8):
-                nc.gpsimd.tensor_scalar(
+                nc.vector.tensor_scalar(
                     out=angle[:, :, w : 2 * w],
                     in0=angle[:, :, 0:w],
                     scalar1=10000.0 ** (-w / FREQS),
                     scalar2=None,
                     op0=ALU.mult,
                 )
-            shifted = keep.tile([P, coords, FREQS], F32)
-            nc.gpsimd.tensor_scalar(
+
+        def whole_turns():
+            nc.vector.tensor_scalar(
                 out=shifted[:], in0=angle[:], scalar1=0.5 / math.pi, scalar2=ROUND, op0=ALU.mult, op1=ALU.add
             )
-            turns = keep.tile([P, coords, FREQS], F32)
-            nc.gpsimd.tensor_scalar(out=turns[:], in0=shifted[:], scalar1=ROUND, scalar2=None, op0=ALU.subtract)
-            rest = angle
+            nc.vector.tensor_scalar(out=turns[:], in0=shifted[:], scalar1=ROUND, scalar2=None, op0=ALU.subtract)
+
+        def take_turns_off():
+            left = angle
             for i, part in enumerate((TURN_HIGH, TURN_LOW)):
-                turned = keep.tile([P, coords, FREQS], F32, name="turned%d" % i)
-                nc.gpsimd.tensor_scalar(out=turned[:], in0=turns[:], scalar1=part, scalar2=0.0, op0=ALU.mult, op1=ALU.add)
-                left = keep.tile([P, coords, FREQS], F32, name="left%d" % i)
-                nc.gpsimd.tensor_tensor(out=left[:], in0=rest[:], in1=turned[:], op=ALU.subtract)
-                rest = left
-            return rest
+                nc.vector.tensor_scalar(out=turned[i][:], in0=turns[:], scalar1=part, scalar2=0.0, op0=ALU.mult, op1=ALU.add)
+                nc.vector.tensor_tensor(out=rest[i][:], in0=left[:], in1=turned[i][:], op=ALU.subtract)
+                left = rest[i]
 
-        def half_and_quarter_sines(rest):
-            sin_half = keep.tile([P, coords, FREQS], F32)
-            nc.scalar.activation(out=sin_half[:], in_=rest[:], func=ACT.Sin, scale=0.5)
-            sin_quarter = keep.tile([P, coords, FREQS], F32)
-            nc.scalar.activation(out=sin_quarter[:], in_=rest[:], func=ACT.Sin, scale=0.25)
-            return sin_half, sin_quarter
+        def half_and_quarter_sines():
+            nc.scalar.activation(out=sin_half[:], in_=rest[1][:], func=ACT.Sin, scale=0.5)
+            nc.scalar.activation(out=sin_quarter[:], in_=rest[1][:], func=ACT.Sin, scale=0.25)
+            root_table = small.tile([P, 1], F32)
+            nc.scalar.activation(out=root_table[:], in_=eps[:], func=ACT.Abs_reciprocal_sqrt)
 
-        def rotary_tables(sin_half, sin_quarter):
-            quarter_sq = keep.tile([P, coords, FREQS], F32)
-            nc.gpsimd.tensor_tensor(out=quarter_sq[:], in0=sin_quarter[:], in1=sin_quarter[:], op=ALU.mult)
-            cos_half = keep.tile([P, coords, FREQS], F32)
-            nc.gpsimd.tensor_scalar(
+        def half_angle_products():
+            nc.vector.tensor_tensor(out=quarter_sq[:], in0=sin_quarter[:], in1=sin_quarter[:], op=ALU.mult)
+            nc.vector.tensor_tensor(out=half_sq[:], in0=sin_half[:], in1=sin_half[:], op=ALU.mult)
+            nc.vector.tensor_scalar(
                 out=cos_half[:], in0=quarter_sq[:], scalar1=-2.0, scalar2=1.0, op0=ALU.mult, op1=ALU.add
             )
-            half_sq = keep.tile([P, coords, FREQS], F32)
-            nc.gpsimd.tensor_tensor(out=half_sq[:], in0=sin_half[:], in1=sin_half[:], op=ALU.mult)
-            half_product = keep.tile([P, coords, FREQS], F32)
-            nc.gpsimd.tensor_tensor(out=half_product[:], in0=sin_half[:], in1=cos_half[:], op=ALU.mult)
+            nc.vector.tensor_tensor(out=half_product[:], in0=sin_half[:], in1=cos_half[:], op=ALU.mult)
+
+        def rotary_tables():
             cos_view = cos_table[:].rearrange("p t (d s j) -> p (t d) s j", d=2, s=2)
             sin_view = sin_table[:].rearrange("p t (d s j) -> p (t d) s j", d=2, s=2)
             for s in range(2):
-                nc.gpsimd.tensor_scalar(
+                nc.vector.tensor_scalar(
                     out=cos_view[:, :, s, :], in0=half_sq[:], scalar1=-2.0, scalar2=1.0, op0=ALU.mult, op1=ALU.add
                 )
-                nc.gpsimd.tensor_scalar(
+                nc.vector.tensor_scalar(
                     out=sin_view[:, :, s, :],
                     in0=half_product[:],
                     scalar1=(-2.0 if s == 0 else 2.0),
@@ -160,7 +165,12 @@ def tile_asymetrickernel_pa_k_kernel(tc, u_x, pos_x, Wk, Wv, out):
                     op0=ALU.mult,
                 )
 
-        rest = reduced_angles()
+        rotary_work = {
+            ROTARY_STEP + i: piece
+            for i, piece in enumerate(
+                (angles, whole_turns, take_turns_off, half_and_quarter_sines, half_angle_products, rotary_tables)
+            )
+        }
 
         def transpose_load(pieces, vector_banks, run):
             grouped = grouped_pool.tile([P, LOAD_PASSES * BANK * 4], BF16, align_bytes=64)
@@ -194,6 +204,16 @@ def tile_asymetrickernel_pa_k_kernel(tc, u_x, pos_x, Wk, Wv, out):
         def quantise(name, pair, grouped):
             cols = slice(pair * LOAD_PASSES * BANK, (pair + 1) * LOAD_PASSES * BANK)
             nc.vector.quantize_mx(out=codes[name][:, cols].bitcast(FP8X4), scales=scales[name][:, cols], in_=grouped[:])
+
+        def quantise_by_pass(name, pair, grouped):
+            for i in range(LOAD_PASSES):
+                c = pair * LOAD_PASSES + i
+                cols = slice(c * BANK, (c + 1) * BANK)
+                nc.vector.quantize_mx(
+                    out=codes[name][:, cols].bitcast(FP8X4),
+                    scales=scales[name][:, cols],
+                    in_=grouped[:, i * BANK * 4 : (i + 1) * BANK * 4],
+                )
 
         def project(acc, weights, c, t, first_channel, n_channels):
             tokens = slice(c * BANK + t * P, c * BANK + (t + 1) * P)
@@ -286,7 +306,7 @@ def tile_asymetrickernel_pa_k_kernel(tc, u_x, pos_x, Wk, Wv, out):
             if step + RAW_BUFS - 1 < len(steps):
                 load(step + RAW_BUFS - 1)
             if waiting is not None:
-                quantise(*waiting)
+                (quantise_by_pass if waiting[1] == 0 else quantise)(*waiting)
                 passes = range(LOAD_PASSES * waiting[1], LOAD_PASSES * (waiting[1] + 1))
                 if waiting[0] == "k":
                     for c in passes:
@@ -302,12 +322,8 @@ def tile_asymetrickernel_pa_k_kernel(tc, u_x, pos_x, Wk, Wv, out):
             vector_banks = 1 if step < v_step + ROW_TILES else 0
             run = MX_RUNS[step % 2] if step < v_step else 4
             waiting = (name, pair, transpose_load(raw_tiles[step], vector_banks, run))
-            if step == SINES_STEP:
-                half_and_quarter = half_and_quarter_sines(rest)
-                root_table = small.tile([P, 1], F32)
-                nc.scalar.activation(out=root_table[:], in_=eps[:], func=ACT.Abs_reciprocal_sqrt)
-            if step == TABLES_STEP:
-                rotary_tables(*half_and_quarter)
+            if step in rotary_work:
+                rotary_work[step]()
             t = step - v_step - 1
             if 0 <= t < ROW_TILES:
                 k_stats[t] = statistics(k_acc[t], HEADS)
@@ -338,38 +354,39 @@ def tile_asymetrickernel_pa_k_kernel(tc, u_x, pos_x, Wk, Wv, out):
         result = keep.tile([P, 2, 2, P], F32)
         out_heads = out[0].rearrange("(f g a) c d -> f a c g d", f=2, g=2)
 
-        def quantise_v(half):
-            cols = slice(half * HALF, (half + 1) * HALF)
-            words = slice(half * HALF * ROW_TILES, (half + 1) * HALF * ROW_TILES)
+        def quantise_v(first, width):
+            words = slice(first * ROW_TILES, (first + width) * ROW_TILES)
+            cols = slice(first, first + width)
             nc.vector.quantize_mx(out=v_codes[:, cols].bitcast(FP8X4), scales=v_scales[:, cols], in_=v_grouped[:, words])
 
-        def finish(half, copies):
-            for g in range(2):
-                pair_cols = slice(half * HALF + g * P, half * HALF + (g + 1) * P)
-                product = psum_work.tile([P, P], F32, tag="bank", name="product")
-                nc.tensor.matmul_mx(
-                    out=product[:],
-                    lhsT=k_codes[:, pair_cols].bitcast(FP8X4),
-                    lhsT_scale=k_scales[:, pair_cols],
-                    rhs=v_codes[:, pair_cols].bitcast(FP8X4),
-                    rhs_scale=v_scales[:, pair_cols],
-                    start=True,
-                    stop=True,
-                )
-                copies[g](out=result[:, half, g, :], in_=product[:])
+        def multiply_pair(pair, copy):
+            cols = slice(pair * P, (pair + 1) * P)
+            product = psum_work.tile([P, P], F32, tag="bank", name="product")
+            nc.tensor.matmul_mx(
+                out=product[:],
+                lhsT=k_codes[:, cols].bitcast(FP8X4),
+                lhsT_scale=k_scales[:, cols],
+                rhs=v_codes[:, cols].bitcast(FP8X4),
+                rhs_scale=v_scales[:, cols],
+                start=True,
+                stop=True,
+            )
+            copy(out=result[:, pair // 2, pair % 2, :], in_=product[:])
+
+        def store(half):
             for a, dma in enumerate((nc.sync.dma_start, nc.scalar.dma_start)):
                 block = slice(a * HEAD, (a + 1) * HEAD)
                 dma(out=out_heads[half, a], in_=result[block, half, :, block])
 
         units = [(t, 0, CHANNELS) for t in range(2)]
-        units += [(t, half * HALF, HALF) for half in range(2) for t in range(2, ROW_TILES)]
+        units += [(2, 0, HALF), (3, 0, HALF), (2, HALF, HALF), (3, HALF, P), (3, HALF + P, P)]
         unnormed = None
         for t, first, width in units:
             if t >= 2:
                 if first == 0:
                     acc = psum_k.tile([P, HALF], F32, tag="acc%d" % t, name="v_acc")
                 else:
-                    acc = psum_work.tile([P, HALF], F32, tag="bank", name="v_acc")
+                    acc = psum_work.tile([P, width], F32, tag="bank", name="v_acc")
                 for c in range(PASSES):
                     project(acc, "v", c, t, first, width)
             else:
@@ -380,8 +397,13 @@ def tile_asymetrickernel_pa_k_kernel(tc, u_x, pos_x, Wk, Wv, out):
             norm = normalise if t < 2 else normalise_on_vector
             unnormed = (acc, width // HEAD, mean, gain, v_words[:, first : first + width, t])
             if (t, first) == (2, HALF):
-                quantise_v(0)
-        finish(0, (nc.scalar.copy, nc.scalar.copy))
+                quantise_v(0, HALF)
+        quantise_v(HALF, P)
+        for pair in range(2):
+            multiply_pair(pair, nc.scalar.copy)
+        store(0)
+        multiply_pair(2, nc.scalar.copy)
         norm(*unnormed)
-        quantise_v(1)
-        finish(1, (nc.vector.tensor_copy, nc.scalar.copy))
+        quantise_v(HALF + P, P)
+        multiply_pair(3, nc.vector.tensor_copy)
+        store(1)

import math
from contextlib import ExitStack

import concourse.mybir as mybir
from concourse.masks import make_identity

F32 = mybir.dt.float32
BF16 = mybir.dt.bfloat16
U32 = mybir.dt.uint32
U8 = mybir.dt.uint8
FP8X4 = mybir.dt.float8_e4m3fn_x4
ALU = mybir.AluOpType
ACT = mybir.ActivationFunctionType

P = 128
TOKENS = 512
DIM = 8192
CHANNELS = 512
HEADS = 8
HEAD = 64
FREQS = 16
ROW_TILES = 4
K_PASS = 512
PASSES = DIM // K_PASS
WORDS = K_PASS // 2
BANK = 512
HALF = CHANNELS // 2
LOAD_PASSES = 2
LOAD_K = LOAD_PASSES * K_PASS
PAIRS = PASSES // LOAD_PASSES
RAW_BUFS = 5
SPLIT_LOADS = 2
MX_RUNS = (4, 3)
LATE_PASSES = 4
ROTARY_STEP = 4
EPS = 1e-5

ROUND = 12582912.0
TURN_HIGH = 6.28125
TURN_LOW = 2.0 * math.pi - TURN_HIGH

FLOPS = 2 * TOKENS * DIM * 2 * CHANNELS + 2 * HEADS * HEAD * HEAD * TOKENS


def tile_asymetrickernel_pa_k_kernel(tc, u_x, pos_x, Wk, Wv, out):
    nc = tc.nc
    with ExitStack() as ctx:
        ctx.enter_context(tc.manual_schedule())
        keep = ctx.enter_context(tc.tile_pool(name="keep", bufs=1))
        raw_pool = ctx.enter_context(tc.tile_pool(name="raw", bufs=RAW_BUFS))
        grouped_pool = ctx.enter_context(tc.tile_pool(name="grouped", bufs=2))
        small = ctx.enter_context(tc.tile_pool(name="small", bufs=ROW_TILES))
        psum_k = ctx.enter_context(tc.psum_pool(name="psum_k", bufs=1))
        psum_work = ctx.enter_context(tc.psum_pool(name="psum_work", bufs=4))

        rows = {
            "x": u_x[0].rearrange("(p t) k -> p t k", t=ROW_TILES),
            "k": Wk.rearrange("(j p) k -> p j k", p=P),
            "v": Wv.rearrange("(j p) k -> p j k", p=P),
        }
        codes = {}
        scales = {}
        for name in ("x", "k", "v"):
            codes[name] = keep.tile([P, PASSES * BANK], U32, name="codes_" + name, align_bytes=64)
            scales[name] = keep.tile([P, PASSES * BANK], U8, name="scales_" + name, align_bytes=64)

        steps = [(name, pair) for pair in range(PAIRS) for name in ("x", "k")]
        v_step = len(steps)
        steps += [("v", pair) for pair in range(PAIRS)]
        raw_tiles = {}

        def load(step):
            name, pair = steps[step]
            raw_tiles[step] = []
            pieces = LOAD_PASSES if step < SPLIT_LOADS else 1
            width = LOAD_K // pieces
            for i in range(pieces):
                bufs = RAW_BUFS if pieces == 1 else SPLIT_LOADS * LOAD_PASSES
                raw = raw_pool.tile([P, ROW_TILES, width], BF16, name="raw%d" % pieces, bufs=bufs)
                first = pair * LOAD_K + i * width
                nc.sync.dma_start(out=raw[:], in_=rows[name][:, :, first : first + width])
                raw_tiles[step].append(raw)

        coords = ROW_TILES * 2
        pos_bf = keep.tile([P, coords], BF16)
        nc.scalar.dma_start(out=pos_bf[:], in_=pos_x[0].rearrange("(p t) d -> p (t d)", t=ROW_TILES))
        for step in range(RAW_BUFS - 1):
            load(step)

        identity = keep.tile([P, P], F32)
        make_identity(nc, identity[:])
        eps = keep.tile([P, 1], F32)
        nc.vector.memset(eps[:], EPS)
        sin_table_load = keep.tile([P, 1], F32)
        nc.scalar.activation(out=sin_table_load[:], in_=eps[:], func=ACT.Sin)

        cos_table = keep.tile([P, ROW_TILES, HEAD], F32)
        sin_table = keep.tile([P, ROW_TILES, HEAD], F32)
        angle = keep.tile([P, coords, FREQS], F32)
        shifted = keep.tile([P, coords, FREQS], F32)
        turns = keep.tile([P, coords, FREQS], F32)
        turned = [keep.tile([P, coords, FREQS], F32, name="turned%d" % i) for i in range(2)]
        rest = [keep.tile([P, coords, FREQS], F32, name="rest%d" % i) for i in range(2)]
        sin_half = keep.tile([P, coords, FREQS], F32)
        sin_quarter = keep.tile([P, coords, FREQS], F32)
        quarter_sq = keep.tile([P, coords, FREQS], F32)
        cos_half = keep.tile([P, coords, FREQS], F32)
        half_sq = keep.tile([P, coords, FREQS], F32)
        half_product = keep.tile([P, coords, FREQS], F32)

        def angles():
            pos = keep.tile([P, coords], F32)
            nc.vector.tensor_copy(out=pos[:], in_=pos_bf[:])
            nc.vector.tensor_scalar(
                out=angle[:, :, 0:1], in0=pos[:].unsqueeze(2), scalar1=64.0, scalar2=None, op0=ALU.mult
            )
            for w in (1, 2, 4, 8):
                nc.vector.tensor_scalar(
                    out=angle[:, :, w : 2 * w],
                    in0=angle[:, :, 0:w],
                    scalar1=10000.0 ** (-w / FREQS),
                    scalar2=None,
                    op0=ALU.mult,
                )

        def whole_turns():
            nc.vector.tensor_scalar(
                out=shifted[:], in0=angle[:], scalar1=0.5 / math.pi, scalar2=ROUND, op0=ALU.mult, op1=ALU.add
            )
            nc.vector.tensor_scalar(out=turns[:], in0=shifted[:], scalar1=ROUND, scalar2=None, op0=ALU.subtract)

        def take_turns_off():
            left = angle
            for i, part in enumerate((TURN_HIGH, TURN_LOW)):
                nc.vector.tensor_scalar(out=turned[i][:], in0=turns[:], scalar1=part, scalar2=0.0, op0=ALU.mult, op1=ALU.add)
                nc.vector.tensor_tensor(out=rest[i][:], in0=left[:], in1=turned[i][:], op=ALU.subtract)
                left = rest[i]

        def half_and_quarter_sines():
            nc.scalar.activation(out=sin_half[:], in_=rest[1][:], func=ACT.Sin, scale=0.5)
            nc.scalar.activation(out=sin_quarter[:], in_=rest[1][:], func=ACT.Sin, scale=0.25)
            root_table = small.tile([P, 1], F32)
            nc.scalar.activation(out=root_table[:], in_=eps[:], func=ACT.Abs_reciprocal_sqrt)

        def half_angle_products():
            nc.vector.tensor_tensor(out=quarter_sq[:], in0=sin_quarter[:], in1=sin_quarter[:], op=ALU.mult)
            nc.vector.tensor_tensor(out=half_sq[:], in0=sin_half[:], in1=sin_half[:], op=ALU.mult)
            nc.vector.tensor_scalar(
                out=cos_half[:], in0=quarter_sq[:], scalar1=-2.0, scalar2=1.0, op0=ALU.mult, op1=ALU.add
            )
            nc.vector.tensor_tensor(out=half_product[:], in0=sin_half[:], in1=cos_half[:], op=ALU.mult)

        def rotary_tables():
            cos_view = cos_table[:].rearrange("p t (d s j) -> p (t d) s j", d=2, s=2)
            sin_view = sin_table[:].rearrange("p t (d s j) -> p (t d) s j", d=2, s=2)
            for s in range(2):
                nc.vector.tensor_scalar(
                    out=cos_view[:, :, s, :], in0=half_sq[:], scalar1=-2.0, scalar2=1.0, op0=ALU.mult, op1=ALU.add
                )
                nc.vector.tensor_scalar(
                    out=sin_view[:, :, s, :],
                    in0=half_product[:],
                    scalar1=(-2.0 if s == 0 else 2.0),
                    scalar2=None,
                    op0=ALU.mult,
                )

        rotary_work = {
            ROTARY_STEP + i: piece
            for i, piece in enumerate(
                (angles, whole_turns, take_turns_off, half_and_quarter_sines, half_angle_products, rotary_tables)
            )
        }

        def transpose_load(pieces, vector_banks, run):
            grouped = grouped_pool.tile([P, LOAD_PASSES * BANK * 4], BF16, align_bytes=64)
            grouped_words = grouped[:].bitcast(F32)
            for b in range(2 * LOAD_PASSES):
                c_local, row_half = divmod(b, 2)
                bank = psum_work.tile([P, BANK], F32)
                for u in range(2):
                    for jj in range(2):
                        if len(pieces) == 1:
                            words, first = pieces[0], c_local * WORDS + u * P
                        else:
                            words, first = pieces[c_local], u * P
                        nc.tensor.transpose(
                            bank[:, (2 * u + jj) * P : (2 * u + jj + 1) * P],
                            words[:, 2 * row_half + jj, :].bitcast(F32)[:, first : first + P],
                            identity[:],
                        )
                copy = nc.scalar.copy if b < 2 * LOAD_PASSES - vector_banks else nc.vector.tensor_copy
                copy(
                    out=grouped_words[:, b * BANK : (b + 1) * BANK].rearrange("p (r u) -> p r u", u=2),
                    in_=bank[:].rearrange("p (u r) -> p r u", u=2),
                )
                if b == LOAD_PASSES - 1:
                    multiply_ready((run + 1) // 2)
                    ready.extend(fresh)
                    fresh.clear()
            multiply_ready(run // 2)
            return grouped

        def quantise(name, pair, grouped):
            cols = slice(pair * LOAD_PASSES * BANK, (pair + 1) * LOAD_PASSES * BANK)
            nc.vector.quantize_mx(out=codes[name][:, cols].bitcast(FP8X4), scales=scales[name][:, cols], in_=grouped[:])

        def quantise_by_pass(name, pair, grouped):
            for i in range(LOAD_PASSES):
                c = pair * LOAD_PASSES + i
                cols = slice(c * BANK, (c + 1) * BANK)
                nc.vector.quantize_mx(
                    out=codes[name][:, cols].bitcast(FP8X4),
                    scales=scales[name][:, cols],
                    in_=grouped[:, i * BANK * 4 : (i + 1) * BANK * 4],
                )

        def project(acc, weights, c, t, first_channel, n_channels):
            tokens = slice(c * BANK + t * P, c * BANK + (t + 1) * P)
            channels = slice(c * BANK + first_channel, c * BANK + first_channel + n_channels)
            nc.tensor.matmul_mx(
                out=acc[:],
                lhsT=codes["x"][:, tokens].bitcast(FP8X4),
                lhsT_scale=scales["x"][:, tokens],
                rhs=codes[weights][:, channels].bitcast(FP8X4),
                rhs_scale=scales[weights][:, channels],
                start=(c == 0),
                stop=(c == PASSES - 1),
            )

        def statistics(acc, heads):
            moments = small.tile([P, heads, 3], F32, name="moments%d" % heads)
            for g in range(heads // 2):
                nc.vector.bn_stats(
                    out=moments[:, 2 * g : 2 * g + 2, :].rearrange("p h m -> p (h m)"),
                    in_=acc[:, 2 * g * HEAD : (2 * g + 2) * HEAD].rearrange("p (h c) -> p c h", h=2),
                )
            gain = small.tile([P, heads], F32, name="gain%d" % heads)
            nc.scalar.activation(
                out=gain[:], in_=moments[:, :, 2], func=ACT.Abs_reciprocal_sqrt, bias=eps[:], scale=1.0 / HEAD
            )
            return moments[:, :, 1], gain

        def normalise_on_vector(acc, heads, mean, gain, normed):
            for h in range(heads):
                head = slice(h * HEAD, (h + 1) * HEAD)
                nc.vector.tensor_scalar(
                    out=normed[:, head],
                    in0=acc[:, head],
                    scalar1=mean[:, h : h + 1],
                    scalar2=gain[:, h : h + 1],
                    op0=ALU.subtract,
                    op1=ALU.mult,
                )

        def normalise(acc, heads, mean, gain, normed):
            shift = small.tile([P, heads], F32, name="shift%d" % heads)
            nc.vector.scalar_tensor_tensor(
                out=shift[:], in0=mean, scalar=-1.0, in1=gain[:], op0=ALU.mult, op1=ALU.mult
            )
            for h in range(heads):
                head = slice(h * HEAD, (h + 1) * HEAD)
                nc.scalar.activation(
                    out=normed[:, head], in_=acc[:, head], func=ACT.Identity, bias=shift[:, h : h + 1], scale=gain[:, h : h + 1]
                )

        k_normed = keep.tile([P, ROW_TILES, CHANNELS], F32)
        crossed = keep.tile([P, ROW_TILES, CHANNELS], F32)

        def rotate(t):
            y = k_normed[:, t, :].rearrange("p (h d s j) -> p h d s j", h=HEADS, d=2, s=2)
            z = crossed[:, t, :].rearrange("p (h d s j) -> p h d s j", h=HEADS, d=2, s=2)
            sines = sin_table[:, t, :].rearrange("p (d s j) -> p d s j", d=2, s=2)
            for s in range(2):
                nc.vector.tensor_tensor(
                    out=z[:, :, :, s, :],
                    in0=y[:, :, :, 1 - s, :],
                    in1=sines[:, :, s, :].unsqueeze(1).to_broadcast([P, HEADS, 2, FREQS]),
                    op=ALU.mult,
                )
            straight = k_normed[:, t, :].rearrange("p (h c) -> p h c", h=HEADS)
            nc.vector.tensor_tensor(
                out=straight,
                in0=straight,
                in1=cos_table[:, t, :].unsqueeze(1).to_broadcast([P, HEADS, HEAD]),
                op=ALU.mult,
            )

        k_acc = [psum_k.tile([P, BANK], F32, name="acc%d" % t) for t in range(ROW_TILES)]
        accs = {("k", t): k_acc[t] for t in range(ROW_TILES)}

        k_stats = {}

        waiting = None
        ready = []
        fresh = []
        late = []

        def multiply_ready(count):
            for weights, c, t in ready[:count]:
                project(accs[weights, t], weights, c, t, 0, CHANNELS)
            for one in ready[:count]:
                ready.remove(one)

        for step, (name, pair) in enumerate(steps):
            if step + RAW_BUFS - 1 < len(steps):
                load(step + RAW_BUFS - 1)
            if waiting is not None:
                (quantise_by_pass if waiting[1] == 0 else quantise)(*waiting)
                passes = range(LOAD_PASSES * waiting[1], LOAD_PASSES * (waiting[1] + 1))
                if waiting[0] == "k":
                    for c in passes:
                        for t in range(ROW_TILES):
                            (fresh if c < PASSES - LATE_PASSES else late).append(("k", c, t))
                    if pair == 0 and name == "v":
                        fresh += sorted(late, key=lambda one: (one[2], one[1]))
                if waiting[0] == "v":
                    fresh += [("v", c, t) for c in passes for t in range(2)]
            if step == v_step + ROW_TILES:
                for t in range(2):
                    accs["v", t] = psum_k.tile([P, BANK], F32, tag="acc%d" % t, name="v_acc")
            vector_banks = 1 if step < v_step + ROW_TILES else 0
            run = MX_RUNS[step % 2] if step < v_step else 4
            waiting = (name, pair, transpose_load(raw_tiles[step], vector_banks, run))
            if step in rotary_work:
                rotary_work[step]()
            t = step - v_step - 1
            if 0 <= t < ROW_TILES:
                k_stats[t] = statistics(k_acc[t], HEADS)
            if 0 <= t - 1 < ROW_TILES:
                normalise(k_acc[t - 1], HEADS, k_stats[t - 1][0], k_stats[t - 1][1], k_normed[:, t - 1, :])
            if 0 <= t - 3 < ROW_TILES:
                rotate(t - 3)
        quantise(*waiting)
        ready += [("v", c, t) for c in range(PASSES - LOAD_PASSES, PASSES) for t in range(2)]
        for weights, c, t in ready:
            project(accs[weights, t], weights, c, t, 0, CHANNELS)

        k_grouped = keep.tile([P, CHANNELS * ROW_TILES], BF16, align_bytes=64)
        nc.vector.tensor_tensor(
            out=k_grouped[:].rearrange("p (c t) -> p c t", t=ROW_TILES),
            in0=k_normed[:].rearrange("p t c -> p c t"),
            in1=crossed[:].rearrange("p t c -> p c t"),
            op=ALU.add,
        )
        k_codes = keep.tile([P, CHANNELS], U32, align_bytes=64)
        k_scales = keep.tile([P, CHANNELS], U8, align_bytes=64)
        nc.vector.quantize_mx(out=k_codes[:].bitcast(FP8X4), scales=k_scales[:], in_=k_grouped[:])

        v_grouped = keep.tile([P, CHANNELS * ROW_TILES], BF16, align_bytes=64)
        v_words = v_grouped[:].rearrange("p (c t) -> p c t", t=ROW_TILES)
        v_codes = keep.tile([P, CHANNELS], U32, align_bytes=64)
        v_scales = keep.tile([P, CHANNELS], U8, align_bytes=64)
        result = keep.tile([P, 2, 2, P], F32)
        out_heads = out[0].rearrange("(f g a) c d -> f a c g d", f=2, g=2)

        def quantise_v(first, width):
            words = slice(first * ROW_TILES, (first + width) * ROW_TILES)
            cols = slice(first, first + width)
            nc.vector.quantize_mx(out=v_codes[:, cols].bitcast(FP8X4), scales=v_scales[:, cols], in_=v_grouped[:, words])

        def multiply_pair(pair, copy):
            cols = slice(pair * P, (pair + 1) * P)
            product = psum_work.tile([P, P], F32, tag="bank", name="product")
            nc.tensor.matmul_mx(
                out=product[:],
                lhsT=k_codes[:, cols].bitcast(FP8X4),
                lhsT_scale=k_scales[:, cols],
                rhs=v_codes[:, cols].bitcast(FP8X4),
                rhs_scale=v_scales[:, cols],
                start=True,
                stop=True,
            )
            copy(out=result[:, pair // 2, pair % 2, :], in_=product[:])

        def store(half):
            for a, dma in enumerate((nc.sync.dma_start, nc.scalar.dma_start)):
                block = slice(a * HEAD, (a + 1) * HEAD)
                dma(out=out_heads[half, a], in_=result[block, half, :, block])

        units = [(t, 0, CHANNELS) for t in range(2)]
        units += [(2, 0, HALF), (3, 0, HALF), (2, HALF, HALF), (3, HALF, P), (3, HALF + P, P)]
        unnormed = None
        for t, first, width in units:
            if t >= 2:
                if first == 0:
                    acc = psum_k.tile([P, HALF], F32, tag="acc%d" % t, name="v_acc")
                else:
                    acc = psum_work.tile([P, width], F32, tag="bank", name="v_acc")
                for c in range(PASSES):
                    project(acc, "v", c, t, first, width)
            else:
                acc = accs["v", t]
            mean, gain = statistics(acc, width // HEAD)
            if unnormed is not None:
                norm(*unnormed)
            norm = normalise if t < 2 else normalise_on_vector
            unnormed = (acc, width // HEAD, mean, gain, v_words[:, first : first + width, t])
            if (t, first) == (2, HALF):
                quantise_v(0, HALF)
        quantise_v(HALF, P)
        for pair in range(2):
            multiply_pair(pair, nc.scalar.copy)
        store(0)
        multiply_pair(2, nc.scalar.copy)
        norm(*unnormed)
        quantise_v(HALF + P, P)
        multiply_pair(3, nc.vector.tensor_copy)
        store(1)
